import numpy as np
import ml_dtypes


def mxq(x, axis, fmt="e4m3"):
    dtype, down = {"e4m3": (ml_dtypes.float8_e4m3fn, 7), "e5m2": (ml_dtypes.float8_e5m2, 14)}[fmt]
    v = np.moveaxis(np.asarray(x, np.float32).astype(ml_dtypes.bfloat16).astype(np.float64), axis, -1)
    blocks = v.reshape(v.shape[:-1] + (-1, 32))
    amax = np.abs(blocks).max(-1, keepdims=True)
    byte = np.maximum(np.where(amax > 0, np.frexp(amax)[1] - 1 + 127, 0) - down, 1)
    scale = np.exp2(byte - 127.0)
    codes = (blocks / scale).astype(np.float32).astype(dtype).astype(np.float64)
    return np.moveaxis((codes * scale).reshape(v.shape), -1, axis)


WIDE = False


def mx_kscale(k):
    if not WIDE:
        return np.ones(k)
    levels = np.array([10, -10, 5, -5, 0])
    a = np.random.permutation(np.resize(levels, k // 512 * 4)).reshape(k // 512, 4)
    idx = np.arange(k)
    return np.exp2(a[idx // 512, idx % 128 // 32])


BF16 = ml_dtypes.bfloat16


def bf(x):
    return np.asarray(x, np.float32).astype(BF16)


def f64(x):
    return np.asarray(x).astype(np.float64)


B, N, D = 16, 512, 256
C = 2 * D
EPS_L1 = 1e-12
EPS_BN = 1e-5
NEG_SLOPE = 0.01


def l1_normalize(x):
    return x / np.maximum(np.sum(np.abs(x), axis=-1, keepdims=True), EPS_L1)


def bn_lrelu(x, g, b):
    mean = np.mean(x, axis=(0, 2), keepdims=True)
    var = np.var(x, axis=(0, 2), keepdims=True)
    y = (x - mean) / np.sqrt(var + EPS_BN) * g[None, :, None] + b[None, :, None]
    return np.where(y >= 0, y, NEG_SLOPE * y)


def draw_edge():
    a = 0.5 * np.random.random_sample((B, N, 1))
    u = (1.0 + a) * np.random.random_sample((B, N, N)) - a + 8.0 * np.eye(N)
    return bf(u * np.exp(0.5 * np.random.standard_normal((B, N, 1))))


def draw_nodes():
    level = (0.5 + np.random.random_sample((B, 1, D))) * np.sign(np.random.standard_normal((B, 1, D)))
    return level + np.random.standard_normal((B, N, D))


def setup_inputs():
    t = mx_kscale(C)[:D]
    tt = np.concatenate([t, t])
    return {"distribution_edge": draw_edge(),
            "instance_edge": draw_edge(),
            "point_node": bf(draw_nodes() * t),
            "W1": bf(np.random.standard_normal((C, C)) * 2.0 / np.sqrt(C) / tt[None, :]),
            "g1": bf(1.0 + 0.2 * np.random.standard_normal(C)),
            "b1": bf(0.3 * np.random.standard_normal(C))}


def reference(distribution_edge, instance_edge, point_node, W1, g1, b1):
    diag_mask = 1.0 - np.eye(N)
    pq = mxq(f64(point_node), 1, "e4m3")
    edge_feat = l1_normalize(f64(distribution_edge) * diag_mask)
    aggr_feat = mxq(edge_feat, 2, "e4m3") @ pq
    edge_instance = l1_normalize(f64(instance_edge) * diag_mask)
    aggr_instance = mxq(edge_instance, 2, "e4m3") @ pq
    x = np.concatenate([aggr_feat, aggr_instance], axis=-1)
    x = np.swapaxes(x, 1, 2)
    z = mxq(f64(W1), 1, "e4m3") @ mxq(x, 1, "e4m3")
    return bn_lrelu(z, f64(g1), f64(b1))

@@ -1,0 +1,255 @@
+from contextlib import ExitStack
+
+import concourse.mybir as mybir
+from concourse.masks import make_identity
+
+F32 = mybir.dt.float32
+BF16 = mybir.dt.bfloat16
+U32 = mybir.dt.uint32
+U8 = mybir.dt.uint8
+FP8X4 = mybir.dt.float8_e4m3fn_x4
+ALU = mybir.AluOpType
+ACT = mybir.ActivationFunctionType
+
+P = 128
+PACK = 4
+B = 16
+N = 512
+D = 256
+C = 2 * D
+KINDS = 2
+ROW_TILES = N // P
+EPS_L1 = 1e-12
+EPS_BN = 1e-5
+NEG_SLOPE = 0.01
+BN_STATS_DIM = 6
+
+FLOPS = 2 * B * (KINDS * N * N * D + C * C * N)
+
+
+def tile_yuyipointupdate_pa_t_kernel(
+    tc, distribution_edge, instance_edge, point_node, W1, g1, b1, out
+):
+    nc = tc.nc
+    edges = (distribution_edge, instance_edge)
+
+    with ExitStack() as ctx:
+        const = ctx.enter_context(tc.tile_pool(name="const", bufs=1))
+        loads = ctx.enter_context(tc.tile_pool(name="loads", bufs=4))
+        work = ctx.enter_context(tc.tile_pool(name="work", bufs=3))
+        small = ctx.enter_context(tc.tile_pool(name="small", bufs=6))
+        outs = ctx.enter_context(tc.tile_pool(name="outs", bufs=2))
+        psum_setup = ctx.enter_context(tc.psum_pool(name="psum_setup", bufs=1))
+        psum_et = ctx.enter_context(tc.psum_pool(name="psum_et", bufs=2))
+        psum_xt = ctx.enter_context(tc.psum_pool(name="psum_xt", bufs=2))
+        psum_z = ctx.enter_context(tc.psum_pool(name="psum_z", bufs=3))
+
+        ident_f32 = const.tile([P, P], F32)
+        make_identity(nc, ident_f32[:])
+        ident_bf16 = const.tile([P, P], BF16)
+        nc.vector.tensor_copy(out=ident_bf16[:], in_=ident_f32[:])
+        offdiag = const.tile([P, P], BF16)
+        nc.vector.tensor_scalar(
+            out=offdiag[:], in0=ident_f32[:], scalar1=-1.0, scalar2=1.0, op0=ALU.mult, op1=ALU.add
+        )
+
+        w_raw = const.tile([P, ROW_TILES, C], BF16)
+        nc.scalar.dma_start(out=w_raw[:], in_=W1.rearrange("(ob p) c -> p ob c", p=P))
+        w_grouped = const.tile([P, ROW_TILES, P, PACK], BF16, align_bytes=64)
+        for ob in range(ROW_TILES):
+            wt_ps = psum_setup.tile([P, PACK, P], BF16, tag="setup")
+            for t in range(PACK):
+                nc.tensor.transpose(
+                    out=wt_ps[:, t, :], in_=w_raw[:, ob, t * P : (t + 1) * P], identity=ident_bf16[:]
+                )
+            nc.vector.tensor_copy(out=w_grouped[:, ob], in_=wt_ps[:].rearrange("p t o -> p o t"))
+        w_codes = const.tile([P, C], U32, align_bytes=64)
+        w_scales = const.tile([P, C], U8, align_bytes=64)
+        nc.vector.quantize_mx(
+            out=w_codes[:].bitcast(FP8X4),
+            scales=w_scales[:],
+            in_=w_grouped[:].rearrange("p ob o t -> p (ob o t)"),
+        )
+
+        gb_rows = const.tile([P, P], BF16)
+        nc.vector.memset(gb_rows[:], 0.0)
+        nc.scalar.dma_start(out=gb_rows[0:ROW_TILES, :], in_=g1.rearrange("(ob p) -> ob p", p=P))
+        nc.scalar.dma_start(
+            out=gb_rows[ROW_TILES : 2 * ROW_TILES, :], in_=b1.rearrange("(ob p) -> ob p", p=P)
+        )
+        gb_ps = psum_setup.tile([P, P], BF16, tag="setup")
+        nc.tensor.transpose(out=gb_ps[:], in_=gb_rows[:], identity=ident_bf16[:])
+        gb_cols = const.tile([P, 2 * ROW_TILES], F32)
+        nc.vector.tensor_copy(out=gb_cols[:], in_=gb_ps[:, 0 : 2 * ROW_TILES])
+
+        x_codes = const.tile([P, B, N], U32, align_bytes=64)
+        x_scales = const.tile([P, B, N], U8, align_bytes=64)
+        stats = const.tile([P, ROW_TILES, B, BN_STATS_DIM], F32)
+        e_abs = const.tile([P, KINDS, ROW_TILES, N], BF16)
+
+        def z_tile(g, ob):
+            z_ps = psum_z.tile([P, N], F32)
+            nc.tensor.matmul_mx(
+                out=z_ps[:],
+                lhsT=w_codes[:, ob * P : (ob + 1) * P].bitcast(FP8X4),
+                lhsT_scale=w_scales[:, ob * P : (ob + 1) * P],
+                rhs=x_codes[:, g, :].bitcast(FP8X4),
+                rhs_scale=x_scales[:, g, :],
+                start=True,
+                stop=True,
+            )
+            return z_ps
+
+        for g in range(B):
+            e_raw = loads.tile([P, KINDS, ROW_TILES, N], BF16)
+            for e in range(KINDS):
+                nc.sync.dma_start(out=e_raw[:, e], in_=edges[e][g].rearrange("(r p) m -> p r m", p=P))
+            p_raw = loads.tile([P, PACK, D], BF16)
+            nc.sync.dma_start(
+                out=p_raw[:].rearrange("p (u i) d -> p u (i d)", u=2),
+                in_=point_node[g].rearrange("(u p i) d -> p u (i d)", u=2, i=2),
+            )
+
+            p_grouped = work.tile([P, D, PACK], BF16, align_bytes=64)
+            nc.vector.tensor_copy(out=p_grouped[:], in_=p_raw[:].rearrange("p t d -> p d t"))
+            p_codes = work.tile([P, D], U32, align_bytes=64)
+            p_scales = work.tile([P, D], U8, align_bytes=64)
+            nc.vector.quantize_mx(
+                out=p_codes[:].bitcast(FP8X4),
+                scales=p_scales[:],
+                in_=p_grouped[:].rearrange("p d t -> p (d t)"),
+            )
+
+            for r in range(ROW_TILES):
+                diag_block = e_raw[:, :, r, r * P : (r + 1) * P]
+                nc.vector.tensor_tensor(
+                    out=diag_block,
+                    in0=diag_block,
+                    in1=offdiag[:].unsqueeze(1).to_broadcast([P, KINDS, P]),
+                    op=ALU.mult,
+                )
+
+            row_sum = small.tile([P, KINDS * ROW_TILES], F32)
+            for e in range(KINDS):
+                for r in range(ROW_TILES):
+                    k = e * ROW_TILES + r
+                    nc.scalar.activation(
+                        out=e_abs[:, e, r, :],
+                        in_=e_raw[:, e, r, :],
+                        func=ACT.Abs,
+                        accum_out=row_sum[:, k : k + 1],
+                    )
+            row_div = small.tile([P, KINDS * ROW_TILES], F32)
+            nc.vector.tensor_scalar_max(out=row_div[:], in0=row_sum[:], scalar1=EPS_L1)
+            row_scale = small.tile([P, KINDS * ROW_TILES], F32)
+            nc.vector.reciprocal(out=row_scale[:], in_=row_div[:])
+
+            e_norm = work.tile([P, KINDS, ROW_TILES, N], BF16)
+            for e in range(KINDS):
+                for r in range(ROW_TILES):
+                    k = e * ROW_TILES + r
+                    nc.vector.tensor_scalar(
+                        out=e_norm[:, e, r, :],
+                        in0=e_raw[:, e, r, :],
+                        scalar1=row_scale[:, k : k + 1],
+                        scalar2=None,
+                        op0=ALU.mult,
+                    )
+
+            e_words = e_norm[:].bitcast(F32)
+            e_grouped = work.tile([P, KINDS, N * PACK], BF16, align_bytes=64)
+            e_grouped_words = e_grouped[:].bitcast(F32)
+            e_codes = work.tile([P, KINDS, N], U32, align_bytes=64)
+            e_scales = work.tile([P, KINDS, N], U8, align_bytes=64)
+            for e in range(KINDS):
+                for h in range(2):
+                    et_ps = psum_et.tile([P, 2, 2 * P], F32)
+                    for rr in range(2):
+                        for u in range(2):
+                            nc.tensor.transpose(
+                                out=et_ps[:, u, rr * P : (rr + 1) * P],
+                                in_=e_words[:, e, 2 * h + rr, u * P : (u + 1) * P],
+                                identity=ident_f32[:],
+                            )
+                    nc.scalar.copy(
+                        out=e_grouped_words[:, e, h * 4 * P : (h + 1) * 4 * P].rearrange(
+                            "p (n u) -> p n u", u=2
+                        ),
+                        in_=et_ps[:].rearrange("p u n -> p n u"),
+                    )
+                nc.vector.quantize_mx(
+                    out=e_codes[:, e, :].bitcast(FP8X4),
+                    scales=e_scales[:, e, :],
+                    in_=e_grouped[:, e, :],
+                )
+
+            x_grouped = work.tile([P, N, PACK], BF16, align_bytes=64)
+            for nb in range(ROW_TILES):
+                xt_ps = psum_xt.tile([P, PACK, P], F32)
+                for e in range(KINDS):
+                    for dh in range(2):
+                        nc.tensor.matmul_mx(
+                            out=xt_ps[:, 2 * e + dh, :],
+                            lhsT=p_codes[:, dh * P : (dh + 1) * P].bitcast(FP8X4),
+                            lhsT_scale=p_scales[:, dh * P : (dh + 1) * P],
+                            rhs=e_codes[:, e, nb * P : (nb + 1) * P].bitcast(FP8X4),
+                            rhs_scale=e_scales[:, e, nb * P : (nb + 1) * P],
+                            start=True,
+                            stop=True,
+                        )
+                copy_out = nc.scalar.copy if nb % 2 == 0 else nc.vector.tensor_copy
+                copy_out(
+                    out=x_grouped[:, nb * P : (nb + 1) * P, :],
+                    in_=xt_ps[:].rearrange("p t n -> p n t"),
+                )
+            nc.vector.quantize_mx(
+                out=x_codes[:, g, :].bitcast(FP8X4),
+                scales=x_scales[:, g, :],
+                in_=x_grouped[:].rearrange("p n t -> p (n t)"),
+            )
+
+            for ob in range(ROW_TILES):
+                z_ps = z_tile(g, ob)
+                nc.vector.bn_stats(out=stats[:, ob, g, :], in_=z_ps[:])
+
+        mean_var = const.tile([P, ROW_TILES, 2], F32)
+        for ob in range(ROW_TILES):
+            nc.vector.bn_aggr(
+                out=mean_var[:, ob, :], in_=stats[:, ob, :, :].rearrange("p g s -> p (g s)")
+            )
+        var_eps = const.tile([P, ROW_TILES], F32)
+        nc.vector.tensor_scalar_add(out=var_eps[:], in0=mean_var[:, :, 1], scalar1=EPS_BN)
+        std = const.tile([P, ROW_TILES], F32)
+        nc.scalar.sqrt(out=std[:], in_=var_eps[:])
+        inv_std = const.tile([P, ROW_TILES], F32)
+        nc.vector.reciprocal(out=inv_std[:], in_=std[:])
+        bn_scale = const.tile([P, ROW_TILES], F32)
+        nc.vector.tensor_mul(out=bn_scale[:], in0=gb_cols[:, 0:ROW_TILES], in1=inv_std[:])
+        mean_scaled = const.tile([P, ROW_TILES], F32)
+        nc.vector.tensor_mul(out=mean_scaled[:], in0=mean_var[:, :, 0], in1=bn_scale[:])
+        bn_shift = const.tile([P, ROW_TILES], F32)
+        nc.vector.tensor_sub(
+            out=bn_shift[:], in0=gb_cols[:, ROW_TILES : 2 * ROW_TILES], in1=mean_scaled[:]
+        )
+
+        for g in range(B):
+            result = outs.tile([P, ROW_TILES, N], F32)
+            for ob in range(ROW_TILES):
+                z_ps = z_tile(g, ob)
+                y = outs.tile([P, N], F32)
+                nc.scalar.activation(
+                    out=y[:],
+                    in_=z_ps[:],
+                    func=ACT.Identity,
+                    scale=bn_scale[:, ob : ob + 1],
+                    bias=bn_shift[:, ob : ob + 1],
+                )
+                nc.vector.scalar_tensor_tensor(
+                    out=result[:, ob, :],
+                    in0=y[:],
+                    scalar=NEG_SLOPE,
+                    in1=y[:],
+                    op0=ALU.mult,
+                    op1=ALU.max,
+                )
+            nc.sync.dma_start(out=out[g].rearrange("(ob p) n -> p ob n", p=P), in_=result[:])

@@ -18,11 +18,30 @@ N = 512
 D = 256
 C = 2 * D
 KINDS = 2
-ROW_TILES = N // P
+QUARTERS = N // P
+PSUM_BANKS = 8
 EPS_L1 = 1e-12
 EPS_BN = 1e-5
 NEG_SLOPE = 0.01
 BN_STATS_DIM = 6
+
+LOAD_AT = -2 * QUARTERS
+MASK_AT = 0
+ABS_AT = MASK_AT + 2
+P_REGROUP_AT = 4
+P_QUANT_AT = P_REGROUP_AT + 2
+ROW_SCALE_AT = ABS_AT + (QUARTERS - 1) + 2
+NORM_AT = ROW_SCALE_AT + 1
+TRANSPOSE_AT = NORM_AT + 1
+E_REGROUP_AT = TRANSPOSE_AT + 1
+E_QUANT_AT = E_REGROUP_AT + 1 + 2
+X_MATMUL_AT = E_QUANT_AT + 2 + 1
+X_REGROUP_AT = X_MATMUL_AT + 1
+X_QUANT_AT = X_REGROUP_AT + (QUARTERS - 1) + 1
+Z_MATMUL_AT = X_QUANT_AT + 1
+Z_STATS_AT = Z_MATMUL_AT + 1
+LAST_STEP = QUARTERS * (B - 1) + Z_STATS_AT + (QUARTERS - 1)
+WEIGHTS_STEP = QUARTERS
 
 FLOPS = 2 * B * (KINDS * N * N * D + C * C * N)
 
@@ -35,14 +54,11 @@ def tile_yuyipointupdate_pa_t_kernel(
 
     with ExitStack() as ctx:
         const = ctx.enter_context(tc.tile_pool(name="const", bufs=1))
-        loads = ctx.enter_context(tc.tile_pool(name="loads", bufs=4))
-        work = ctx.enter_context(tc.tile_pool(name="work", bufs=3))
-        small = ctx.enter_context(tc.tile_pool(name="small", bufs=6))
-        outs = ctx.enter_context(tc.tile_pool(name="outs", bufs=2))
-        psum_setup = ctx.enter_context(tc.psum_pool(name="psum_setup", bufs=1))
-        psum_et = ctx.enter_context(tc.psum_pool(name="psum_et", bufs=2))
-        psum_xt = ctx.enter_context(tc.psum_pool(name="psum_xt", bufs=2))
-        psum_z = ctx.enter_context(tc.psum_pool(name="psum_z", bufs=3))
+        pipe2 = ctx.enter_context(tc.tile_pool(name="pipe2", bufs=2))
+        pipe3 = ctx.enter_context(tc.tile_pool(name="pipe3", bufs=3))
+        pipe4 = ctx.enter_context(tc.tile_pool(name="pipe4", bufs=4))
+        psum = ctx.enter_context(tc.psum_pool(name="psum", bufs=PSUM_BANKS))
+        ctx.enter_context(tc.manual_schedule())
 
         ident_f32 = const.tile([P, P], F32)
         make_identity(nc, ident_f32[:])
@@ -52,45 +68,54 @@ def tile_yuyipointupdate_pa_t_kernel(
         nc.vector.tensor_scalar(
             out=offdiag[:], in0=ident_f32[:], scalar1=-1.0, scalar2=1.0, op0=ALU.mult, op1=ALU.add
         )
+        one = const.tile([P, 1], F32)
+        nc.vector.memset(one[:], 1.0)
+        sqrt_of_one = const.tile([P, 1], F32)
+        nc.scalar.sqrt(out=sqrt_of_one[:], in_=one[:])
 
-        w_raw = const.tile([P, ROW_TILES, C], BF16)
-        nc.scalar.dma_start(out=w_raw[:], in_=W1.rearrange("(ob p) c -> p ob c", p=P))
-        w_grouped = const.tile([P, ROW_TILES, P, PACK], BF16, align_bytes=64)
-        for ob in range(ROW_TILES):
-            wt_ps = psum_setup.tile([P, PACK, P], BF16, tag="setup")
-            for t in range(PACK):
-                nc.tensor.transpose(
-                    out=wt_ps[:, t, :], in_=w_raw[:, ob, t * P : (t + 1) * P], identity=ident_bf16[:]
-                )
-            nc.vector.tensor_copy(out=w_grouped[:, ob], in_=wt_ps[:].rearrange("p t o -> p o t"))
+        w_raw = const.tile([P, QUARTERS, C], BF16)
+        w_grouped = const.tile([P, QUARTERS, P, PACK], BF16, align_bytes=64)
         w_codes = const.tile([P, C], U32, align_bytes=64)
         w_scales = const.tile([P, C], U8, align_bytes=64)
-        nc.vector.quantize_mx(
-            out=w_codes[:].bitcast(FP8X4),
-            scales=w_scales[:],
-            in_=w_grouped[:].rearrange("p ob o t -> p (ob o t)"),
-        )
-
         gb_rows = const.tile([P, P], BF16)
         nc.vector.memset(gb_rows[:], 0.0)
-        nc.scalar.dma_start(out=gb_rows[0:ROW_TILES, :], in_=g1.rearrange("(ob p) -> ob p", p=P))
-        nc.scalar.dma_start(
-            out=gb_rows[ROW_TILES : 2 * ROW_TILES, :], in_=b1.rearrange("(ob p) -> ob p", p=P)
-        )
-        gb_ps = psum_setup.tile([P, P], BF16, tag="setup")
-        nc.tensor.transpose(out=gb_ps[:], in_=gb_rows[:], identity=ident_bf16[:])
-        gb_cols = const.tile([P, 2 * ROW_TILES], F32)
-        nc.vector.tensor_copy(out=gb_cols[:], in_=gb_ps[:, 0 : 2 * ROW_TILES])
+        gb_cols = const.tile([P, 2 * QUARTERS], F32)
+
+        def load_weights():
+            nc.sync.dma_start(out=w_raw[:], in_=W1.rearrange("(ob p) c -> p ob c", p=P))
+            nc.sync.dma_start(out=gb_rows[0:QUARTERS, :], in_=g1.rearrange("(ob p) -> ob p", p=P))
+            nc.sync.dma_start(
+                out=gb_rows[QUARTERS : 2 * QUARTERS, :], in_=b1.rearrange("(ob p) -> ob p", p=P)
+            )
+
+        def prepare_weights():
+            for ob in range(QUARTERS):
+                wt_ps = psum.tile([P, PACK, P], BF16, tag="bank")
+                for t in range(PACK):
+                    nc.tensor.transpose(
+                        out=wt_ps[:, t, :],
+                        in_=w_raw[:, ob, t * P : (t + 1) * P],
+                        identity=ident_bf16[:],
+                    )
+                nc.vector.tensor_copy(out=w_grouped[:, ob], in_=wt_ps[:].rearrange("p t o -> p o t"))
+            gb_ps = psum.tile([P, P], BF16, tag="bank")
+            nc.tensor.transpose(out=gb_ps[:], in_=gb_rows[:], identity=ident_bf16[:])
+            nc.vector.tensor_copy(out=gb_cols[:], in_=gb_ps[:, 0 : 2 * QUARTERS])
+            nc.vector.quantize_mx(
+                out=w_codes[:].bitcast(FP8X4),
+                scales=w_scales[:],
+                in_=w_grouped[:].rearrange("p ob o t -> p (ob o t)"),
+            )
 
         x_codes = const.tile([P, B, N], U32, align_bytes=64)
         x_scales = const.tile([P, B, N], U8, align_bytes=64)
-        stats = const.tile([P, ROW_TILES, B, BN_STATS_DIM], F32)
-        e_abs = const.tile([P, KINDS, ROW_TILES, N], BF16)
+        stats = const.tile([P, QUARTERS, B, BN_STATS_DIM], F32)
+        e_abs = const.tile([P, KINDS, QUARTERS, N], BF16)
 
-        def z_tile(g, ob):
-            z_ps = psum_z.tile([P, N], F32)
+        def z_matmul(g, ob):
+            z_bank = psum.tile([P, N], F32, tag="bank")
             nc.tensor.matmul_mx(
-                out=z_ps[:],
+                out=z_bank[:],
                 lhsT=w_codes[:, ob * P : (ob + 1) * P].bitcast(FP8X4),
                 lhsT_scale=w_scales[:, ob * P : (ob + 1) * P],
                 rhs=x_codes[:, g, :].bitcast(FP8X4),
@@ -98,148 +123,237 @@ def tile_yuyipointupdate_pa_t_kernel(
                 start=True,
                 stop=True,
             )
-            return z_ps
+            return z_bank
 
-        for g in range(B):
-            e_raw = loads.tile([P, KINDS, ROW_TILES, N], BF16)
+        e_raw, p_raw, p_grouped, p_codes, p_scales = {}, {}, {}, {}, {}
+        row_sum, row_div, row_scale, e_norm = {}, {}, {}, {}
+        e_grouped, e_codes, e_scales = {}, {}, {}
+        et_ps, xt_ps, x_grouped, z_ps = {}, {}, {}, {}
+
+        def load(g):
+            e_raw[g] = pipe4.tile([P, KINDS, QUARTERS, N], BF16, name="e_raw")
             for e in range(KINDS):
-                nc.sync.dma_start(out=e_raw[:, e], in_=edges[e][g].rearrange("(r p) m -> p r m", p=P))
-            p_raw = loads.tile([P, PACK, D], BF16)
+                nc.sync.dma_start(
+                    out=e_raw[g][:, e], in_=edges[e][g].rearrange("(r p) m -> p r m", p=P)
+                )
+            p_raw[g] = pipe3.tile([P, PACK, D], BF16, name="p_raw")
             nc.sync.dma_start(
-                out=p_raw[:].rearrange("p (u i) d -> p u (i d)", u=2),
+                out=p_raw[g][:].rearrange("p (u i) d -> p u (i d)", u=2),
                 in_=point_node[g].rearrange("(u p i) d -> p u (i d)", u=2, i=2),
             )
 
-            p_grouped = work.tile([P, D, PACK], BF16, align_bytes=64)
-            nc.vector.tensor_copy(out=p_grouped[:], in_=p_raw[:].rearrange("p t d -> p d t"))
-            p_codes = work.tile([P, D], U32, align_bytes=64)
-            p_scales = work.tile([P, D], U8, align_bytes=64)
-            nc.vector.quantize_mx(
-                out=p_codes[:].bitcast(FP8X4),
-                scales=p_scales[:],
-                in_=p_grouped[:].rearrange("p d t -> p (d t)"),
+        def mask_diagonal(g, r):
+            diag_block = e_raw[g][:, :, r, r * P : (r + 1) * P]
+            nc.vector.tensor_tensor(
+                out=diag_block,
+                in0=diag_block,
+                in1=offdiag[:].unsqueeze(1).to_broadcast([P, KINDS, P]),
+                op=ALU.mult,
             )
 
-            for r in range(ROW_TILES):
-                diag_block = e_raw[:, :, r, r * P : (r + 1) * P]
-                nc.vector.tensor_tensor(
-                    out=diag_block,
-                    in0=diag_block,
-                    in1=offdiag[:].unsqueeze(1).to_broadcast([P, KINDS, P]),
-                    op=ALU.mult,
+        def sum_rows(g, r):
+            if r == 0:
+                row_sum[g] = pipe4.tile([P, KINDS * QUARTERS], F32, name="row_sum")
+            for e in range(KINDS):
+                k = e * QUARTERS + r
+                nc.scalar.activation(
+                    out=e_abs[:, e, r, :],
+                    in_=e_raw[g][:, e, r, :],
+                    func=ACT.Abs,
+                    accum_out=row_sum[g][:, k : k + 1],
                 )
 
-            row_sum = small.tile([P, KINDS * ROW_TILES], F32)
-            for e in range(KINDS):
-                for r in range(ROW_TILES):
-                    k = e * ROW_TILES + r
-                    nc.scalar.activation(
-                        out=e_abs[:, e, r, :],
-                        in_=e_raw[:, e, r, :],
-                        func=ACT.Abs,
-                        accum_out=row_sum[:, k : k + 1],
-                    )
-            row_div = small.tile([P, KINDS * ROW_TILES], F32)
-            nc.vector.tensor_scalar_max(out=row_div[:], in0=row_sum[:], scalar1=EPS_L1)
-            row_scale = small.tile([P, KINDS * ROW_TILES], F32)
-            nc.vector.reciprocal(out=row_scale[:], in_=row_div[:])
+        def regroup_nodes(g):
+            p_grouped[g] = pipe2.tile([P, D, PACK], BF16, name="p_grouped", align_bytes=64)
+            nc.vector.tensor_copy(out=p_grouped[g][:], in_=p_raw[g][:].rearrange("p t d -> p d t"))
 
-            e_norm = work.tile([P, KINDS, ROW_TILES, N], BF16)
-            for e in range(KINDS):
-                for r in range(ROW_TILES):
-                    k = e * ROW_TILES + r
-                    nc.vector.tensor_scalar(
-                        out=e_norm[:, e, r, :],
-                        in0=e_raw[:, e, r, :],
-                        scalar1=row_scale[:, k : k + 1],
-                        scalar2=None,
-                        op0=ALU.mult,
-                    )
+        def quantise_nodes(g):
+            p_codes[g] = pipe4.tile([P, D], U32, name="p_codes", align_bytes=64)
+            p_scales[g] = pipe4.tile([P, D], U8, name="p_scales", align_bytes=64)
+            nc.vector.quantize_mx(
+                out=p_codes[g][:].bitcast(FP8X4),
+                scales=p_scales[g][:],
+                in_=p_grouped[g][:].rearrange("p d t -> p (d t)"),
+            )
 
-            e_words = e_norm[:].bitcast(F32)
-            e_grouped = work.tile([P, KINDS, N * PACK], BF16, align_bytes=64)
-            e_grouped_words = e_grouped[:].bitcast(F32)
-            e_codes = work.tile([P, KINDS, N], U32, align_bytes=64)
-            e_scales = work.tile([P, KINDS, N], U8, align_bytes=64)
-            for e in range(KINDS):
-                for h in range(2):
-                    et_ps = psum_et.tile([P, 2, 2 * P], F32)
-                    for rr in range(2):
-                        for u in range(2):
-                            nc.tensor.transpose(
-                                out=et_ps[:, u, rr * P : (rr + 1) * P],
-                                in_=e_words[:, e, 2 * h + rr, u * P : (u + 1) * P],
-                                identity=ident_f32[:],
-                            )
-                    nc.scalar.copy(
-                        out=e_grouped_words[:, e, h * 4 * P : (h + 1) * 4 * P].rearrange(
-                            "p (n u) -> p n u", u=2
-                        ),
-                        in_=et_ps[:].rearrange("p u n -> p n u"),
-                    )
-                nc.vector.quantize_mx(
-                    out=e_codes[:, e, :].bitcast(FP8X4),
-                    scales=e_scales[:, e, :],
-                    in_=e_grouped[:, e, :],
+        def clamp_row_sums(g):
+            row_div[g] = pipe4.tile([P, KINDS * QUARTERS], F32, name="row_div")
+            nc.vector.tensor_scalar_max(out=row_div[g][:], in0=row_sum[g][:], scalar1=EPS_L1)
+
+        def invert_row_sums(g):
+            row_scale[g] = pipe4.tile([P, KINDS * QUARTERS], F32, name="row_scale")
+            nc.vector.reciprocal(out=row_scale[g][:], in_=row_div[g][:])
+
+        def normalise_rows(g, j):
+            e, h = divmod(j, 2)
+            if j == 0:
+                e_norm[g] = pipe2.tile([P, KINDS, QUARTERS, N], BF16, name="e_norm")
+            for r in (2 * h, 2 * h + 1):
+                k = e * QUARTERS + r
+                nc.vector.tensor_scalar(
+                    out=e_norm[g][:, e, r, :],
+                    in0=e_raw[g][:, e, r, :],
+                    scalar1=row_scale[g][:, k : k + 1],
+                    scalar2=None,
+                    op0=ALU.mult,
                 )
 
-            x_grouped = work.tile([P, N, PACK], BF16, align_bytes=64)
-            for nb in range(ROW_TILES):
-                xt_ps = psum_xt.tile([P, PACK, P], F32)
-                for e in range(KINDS):
-                    for dh in range(2):
-                        nc.tensor.matmul_mx(
-                            out=xt_ps[:, 2 * e + dh, :],
-                            lhsT=p_codes[:, dh * P : (dh + 1) * P].bitcast(FP8X4),
-                            lhsT_scale=p_scales[:, dh * P : (dh + 1) * P],
-                            rhs=e_codes[:, e, nb * P : (nb + 1) * P].bitcast(FP8X4),
-                            rhs_scale=e_scales[:, e, nb * P : (nb + 1) * P],
-                            start=True,
-                            stop=True,
-                        )
-                copy_out = nc.scalar.copy if nb % 2 == 0 else nc.vector.tensor_copy
-                copy_out(
-                    out=x_grouped[:, nb * P : (nb + 1) * P, :],
-                    in_=xt_ps[:].rearrange("p t n -> p n t"),
-                )
+        def transpose_rows(g, j):
+            e, h = divmod(j, 2)
+            e_words = e_norm[g][:].bitcast(F32)
+            et_ps[g, j] = psum.tile([P, 2, 2 * P], F32, name="et_ps", tag="bank")
+            for rr in range(2):
+                for u in range(2):
+                    nc.tensor.transpose(
+                        out=et_ps[g, j][:, u, rr * P : (rr + 1) * P],
+                        in_=e_words[:, e, 2 * h + rr, u * P : (u + 1) * P],
+                        identity=ident_f32[:],
+                    )
+
+        def regroup_edges(g, j):
+            e, h = divmod(j, 2)
+            if j == 0:
+                e_grouped[g] = pipe2.tile([P, KINDS, N * PACK], BF16, name="e_grouped", align_bytes=64)
+            e_grouped_words = e_grouped[g][:].bitcast(F32)
+            nc.scalar.copy(
+                out=e_grouped_words[:, e, h * 4 * P : (h + 1) * 4 * P].rearrange(
+                    "p (n u) -> p n u", u=2
+                ),
+                in_=et_ps[g, j][:].rearrange("p u n -> p n u"),
+            )
+
+        def quantise_edges(g, e):
+            if e == 0:
+                e_codes[g] = pipe2.tile([P, KINDS, N], U32, name="e_codes", align_bytes=64)
+                e_scales[g] = pipe2.tile([P, KINDS, N], U8, name="e_scales", align_bytes=64)
+            nc.vector.quantize_mx(
+                out=e_codes[g][:, e, :].bitcast(FP8X4),
+                scales=e_scales[g][:, e, :],
+                in_=e_grouped[g][:, e, :],
+            )
+
+        def x_matmul(g, nb):
+            xt_ps[g, nb] = psum.tile([P, PACK, P], F32, name="xt_ps", tag="bank")
+            for e in range(KINDS):
+                for dh in range(2):
+                    nc.tensor.matmul_mx(
+                        out=xt_ps[g, nb][:, 2 * e + dh, :],
+                        lhsT=p_codes[g][:, dh * P : (dh + 1) * P].bitcast(FP8X4),
+                        lhsT_scale=p_scales[g][:, dh * P : (dh + 1) * P],
+                        rhs=e_codes[g][:, e, nb * P : (nb + 1) * P].bitcast(FP8X4),
+                        rhs_scale=e_scales[g][:, e, nb * P : (nb + 1) * P],
+                        start=True,
+                        stop=True,
+                    )
+
+        def regroup_x(g, nb):
+            if nb == 0:
+                x_grouped[g] = pipe2.tile([P, N, PACK], BF16, name="x_grouped", align_bytes=64)
+            copy_out = nc.scalar.copy if nb % 2 == 0 else nc.vector.tensor_copy
+            copy_out(
+                out=x_grouped[g][:, nb * P : (nb + 1) * P, :],
+                in_=xt_ps[g, nb][:].rearrange("p t n -> p n t"),
+            )
+
+        def quantise_x(g):
             nc.vector.quantize_mx(
                 out=x_codes[:, g, :].bitcast(FP8X4),
                 scales=x_scales[:, g, :],
-                in_=x_grouped[:].rearrange("p n t -> p (n t)"),
+                in_=x_grouped[g][:].rearrange("p n t -> p (n t)"),
             )
 
-            for ob in range(ROW_TILES):
-                z_ps = z_tile(g, ob)
-                nc.vector.bn_stats(out=stats[:, ob, g, :], in_=z_ps[:])
+        def z_first(g, ob):
+            z_ps[g, ob] = z_matmul(g, ob)
 
-        mean_var = const.tile([P, ROW_TILES, 2], F32)
-        for ob in range(ROW_TILES):
+        def z_statistics(g, ob):
+            nc.vector.bn_stats(out=stats[:, ob, g, :], in_=z_ps[g, ob][:])
+
+        def due(step, first_step):
+            g, q = divmod(step - first_step, QUARTERS)
+            return (g, q) if 0 <= g < B else (None, q)
+
+        for step in range(LOAD_AT, LAST_STEP + 1):
+            g, q = due(step, ROW_SCALE_AT)
+            if g is not None and q == 0:
+                clamp_row_sums(g)
+            g, q = due(step, Z_STATS_AT)
+            if g is not None:
+                z_statistics(g, q)
+            g, q = due(step, Z_MATMUL_AT)
+            if g is not None:
+                z_first(g, q)
+            g, q = due(step, X_QUANT_AT)
+            if g is not None and q == 0:
+                quantise_x(g)
+            g, q = due(step, X_REGROUP_AT)
+            if g is not None:
+                regroup_x(g, q)
+            g, q = due(step, X_MATMUL_AT)
+            if g is not None:
+                x_matmul(g, q)
+            g, q = due(step, E_QUANT_AT)
+            if g is not None and q % 2 == 0:
+                quantise_edges(g, q // 2)
+            g, q = due(step, E_REGROUP_AT)
+            if g is not None:
+                regroup_edges(g, q)
+            g, q = due(step, TRANSPOSE_AT)
+            if g is not None:
+                transpose_rows(g, q)
+            g, q = due(step, NORM_AT)
+            if g is not None:
+                normalise_rows(g, q)
+            g, q = due(step, ABS_AT)
+            if g is not None:
+                sum_rows(g, q)
+            if step == WEIGHTS_STEP:
+                prepare_weights()
+            g, q = due(step, MASK_AT)
+            if g is not None:
+                mask_diagonal(g, q)
+            g, q = due(step, P_QUANT_AT)
+            if g is not None and q == 0:
+                quantise_nodes(g)
+            g, q = due(step, P_REGROUP_AT)
+            if g is not None and q == 0:
+                regroup_nodes(g)
+            g, q = due(step, ROW_SCALE_AT)
+            if g is not None and q == 0:
+                invert_row_sums(g)
+            g, q = due(step, LOAD_AT)
+            if g is not None and q == 0:
+                load(g)
+                if g == 0:
+                    load_weights()
+
+        mean_var = const.tile([P, QUARTERS, 2], F32)
+        for ob in range(QUARTERS):
             nc.vector.bn_aggr(
                 out=mean_var[:, ob, :], in_=stats[:, ob, :, :].rearrange("p g s -> p (g s)")
             )
-        var_eps = const.tile([P, ROW_TILES], F32)
+        var_eps = const.tile([P, QUARTERS], F32)
         nc.vector.tensor_scalar_add(out=var_eps[:], in0=mean_var[:, :, 1], scalar1=EPS_BN)
-        std = const.tile([P, ROW_TILES], F32)
+        std = const.tile([P, QUARTERS], F32)
         nc.scalar.sqrt(out=std[:], in_=var_eps[:])
-        inv_std = const.tile([P, ROW_TILES], F32)
+        inv_std = const.tile([P, QUARTERS], F32)
         nc.vector.reciprocal(out=inv_std[:], in_=std[:])
-        bn_scale = const.tile([P, ROW_TILES], F32)
-        nc.vector.tensor_mul(out=bn_scale[:], in0=gb_cols[:, 0:ROW_TILES], in1=inv_std[:])
-        mean_scaled = const.tile([P, ROW_TILES], F32)
+        bn_scale = const.tile([P, QUARTERS], F32)
+        nc.vector.tensor_mul(out=bn_scale[:], in0=gb_cols[:, 0:QUARTERS], in1=inv_std[:])
+        mean_scaled = const.tile([P, QUARTERS], F32)
         nc.vector.tensor_mul(out=mean_scaled[:], in0=mean_var[:, :, 0], in1=bn_scale[:])
-        bn_shift = const.tile([P, ROW_TILES], F32)
+        bn_shift = const.tile([P, QUARTERS], F32)
         nc.vector.tensor_sub(
-            out=bn_shift[:], in0=gb_cols[:, ROW_TILES : 2 * ROW_TILES], in1=mean_scaled[:]
+            out=bn_shift[:], in0=gb_cols[:, QUARTERS : 2 * QUARTERS], in1=mean_scaled[:]
         )
 
         for g in range(B):
-            result = outs.tile([P, ROW_TILES, N], F32)
-            for ob in range(ROW_TILES):
-                z_ps = z_tile(g, ob)
-                y = outs.tile([P, N], F32)
+            result = pipe3.tile([P, QUARTERS, N], F32)
+            for ob in range(QUARTERS):
+                z_again = z_matmul(g, ob)
+                y = pipe4.tile([P, N], F32)
                 nc.scalar.activation(
                     out=y[:],
-                    in_=z_ps[:],
+                    in_=z_again[:],
                     func=ACT.Identity,
                     scale=bn_scale[:, ob : ob + 1],
                     bias=bn_shift[:, ob : ob + 1],

@@ -42,6 +42,8 @@ Z_MATMUL_AT = X_QUANT_AT + 1
 Z_STATS_AT = Z_MATMUL_AT + 1
 LAST_STEP = QUARTERS * (B - 1) + Z_STATS_AT + (QUARTERS - 1)
 WEIGHTS_STEP = QUARTERS
+FILL_GRAPHS = 3
+DRAIN_GRAPHS = 4
 
 FLOPS = 2 * B * (KINDS * N * N * D + C * C * N)
 
@@ -215,7 +217,8 @@ def tile_yuyipointupdate_pa_t_kernel(
             if j == 0:
                 e_grouped[g] = pipe2.tile([P, KINDS, N * PACK], BF16, name="e_grouped", align_bytes=64)
             e_grouped_words = e_grouped[g][:].bitcast(F32)
-            nc.scalar.copy(
+            copy_out = nc.vector.tensor_copy if g < FILL_GRAPHS else nc.scalar.copy
+            copy_out(
                 out=e_grouped_words[:, e, h * 4 * P : (h + 1) * 4 * P].rearrange(
                     "p (n u) -> p n u", u=2
                 ),
@@ -249,7 +252,8 @@ def tile_yuyipointupdate_pa_t_kernel(
         def regroup_x(g, nb):
             if nb == 0:
                 x_grouped[g] = pipe2.tile([P, N, PACK], BF16, name="x_grouped", align_bytes=64)
-            copy_out = nc.scalar.copy if nb % 2 == 0 else nc.vector.tensor_copy
+            on_scalar = nb % 2 == 0 or g >= B - DRAIN_GRAPHS
+            copy_out = nc.scalar.copy if on_scalar else nc.vector.tensor_copy
             copy_out(
                 out=x_grouped[g][:, nb * P : (nb + 1) * P, :],
                 in_=xt_ps[g, nb][:].rearrange("p t n -> p n t"),

@@ -79,16 +79,13 @@ def tile_yuyipointupdate_pa_t_kernel(
         w_grouped = const.tile([P, QUARTERS, P, PACK], BF16, align_bytes=64)
         w_codes = const.tile([P, C], U32, align_bytes=64)
         w_scales = const.tile([P, C], U8, align_bytes=64)
-        gb_rows = const.tile([P, P], BF16)
-        nc.vector.memset(gb_rows[:], 0.0)
+        gb_raw = const.tile([P, 2, 16], BF16)
         gb_cols = const.tile([P, 2 * QUARTERS], F32)
 
         def load_weights():
-            nc.sync.dma_start(out=w_raw[:], in_=W1.rearrange("(ob p) c -> p ob c", p=P))
-            nc.sync.dma_start(out=gb_rows[0:QUARTERS, :], in_=g1.rearrange("(ob p) -> ob p", p=P))
-            nc.sync.dma_start(
-                out=gb_rows[QUARTERS : 2 * QUARTERS, :], in_=b1.rearrange("(ob p) -> ob p", p=P)
-            )
+            nc.sync.dma_start(out=w_raw[:], in_=W1.rearrange("(p ob) c -> p ob c", p=P))
+            nc.sync.dma_start(out=gb_raw[:, 0, 0:QUARTERS], in_=g1.rearrange("(p ob) -> p ob", p=P))
+            nc.sync.dma_start(out=gb_raw[:, 1, 0:QUARTERS], in_=b1.rearrange("(p ob) -> p ob", p=P))
 
         def prepare_weights():
             for ob in range(QUARTERS):
@@ -100,9 +97,9 @@ def tile_yuyipointupdate_pa_t_kernel(
                         identity=ident_bf16[:],
                     )
                 nc.vector.tensor_copy(out=w_grouped[:, ob], in_=wt_ps[:].rearrange("p t o -> p o t"))
-            gb_ps = psum.tile([P, P], BF16, tag="bank")
-            nc.tensor.transpose(out=gb_ps[:], in_=gb_rows[:], identity=ident_bf16[:])
-            nc.vector.tensor_copy(out=gb_cols[:], in_=gb_ps[:, 0 : 2 * QUARTERS])
+            nc.vector.tensor_copy(
+                out=gb_cols[:].rearrange("p (k ob) -> p k ob", k=2), in_=gb_raw[:, :, 0:QUARTERS]
+            )
             nc.vector.quantize_mx(
                 out=w_codes[:].bitcast(FP8X4),
                 scales=w_scales[:],
@@ -370,4 +367,4 @@ def tile_yuyipointupdate_pa_t_kernel(
                     op0=ALU.mult,
                     op1=ALU.max,
                 )
-            nc.sync.dma_start(out=out[g].rearrange("(ob p) n -> p ob n", p=P), in_=result[:])
+            nc.sync.dma_start(out=out[g].rearrange("(p ob) n -> p ob n", p=P), in_=result[:])

@@ -131,10 +131,13 @@ def tile_yuyipointupdate_pa_t_kernel(
 
         def load(g):
             e_raw[g] = pipe4.tile([P, KINDS, QUARTERS, N], BF16, name="e_raw")
-            for e in range(KINDS):
-                nc.sync.dma_start(
-                    out=e_raw[g][:, e], in_=edges[e][g].rearrange("(r p) m -> p r m", p=P)
-                )
+            chunk = 1 if g == 0 else QUARTERS
+            for r in range(0, QUARTERS, chunk):
+                for e in range(KINDS):
+                    nc.sync.dma_start(
+                        out=e_raw[g][:, e, r : r + chunk],
+                        in_=edges[e][g].rearrange("(r p) m -> p r m", p=P)[:, r : r + chunk],
+                    )
             p_raw[g] = pipe3.tile([P, PACK, D], BF16, name="p_raw")
             nc.sync.dma_start(
                 out=p_raw[g][:].rearrange("p (u i) d -> p u (i d)", u=2),
@@ -249,7 +252,7 @@ def tile_yuyipointupdate_pa_t_kernel(
         def regroup_x(g, nb):
             if nb == 0:
                 x_grouped[g] = pipe2.tile([P, N, PACK], BF16, name="x_grouped", align_bytes=64)
-            on_scalar = nb % 2 == 0 or g >= B - DRAIN_GRAPHS
+            on_scalar = nb % 2 == 0 or (nb == 1 and g % 2 == 1) or g >= B - DRAIN_GRAPHS
             copy_out = nc.scalar.copy if on_scalar else nc.vector.tensor_copy
             copy_out(
                 out=x_grouped[g][:, nb * P : (nb + 1) * P, :],
@@ -367,4 +370,10 @@ def tile_yuyipointupdate_pa_t_kernel(
                     op0=ALU.mult,
                     op1=ALU.max,
                 )
-            nc.sync.dma_start(out=out[g].rearrange("(p ob) n -> p ob n", p=P), in_=result[:])
+                stored = 1 if g in (0, B - 1) else 2
+                if (ob + 1) % stored == 0:
+                    blocks = slice(ob + 1 - stored, ob + 1)
+                    nc.sync.dma_start(
+                        out=out[g].rearrange("(p ob) n -> p ob n", p=P)[:, blocks],
+                        in_=result[:, blocks],
+                    )

@@ -28,8 +28,8 @@ BN_STATS_DIM = 6
 LOAD_AT = -2 * QUARTERS
 MASK_AT = 0
 ABS_AT = MASK_AT + 2
-P_REGROUP_AT = 4
-P_QUANT_AT = P_REGROUP_AT + 2
+P_QUANT_AT = 6
+P_REGROUP_AT = P_QUANT_AT - QUARTERS
 ROW_SCALE_AT = ABS_AT + (QUARTERS - 1) + 2
 NORM_AT = ROW_SCALE_AT + 1
 TRANSPOSE_AT = NORM_AT + 1
@@ -124,7 +124,7 @@ def tile_yuyipointupdate_pa_t_kernel(
             )
             return z_bank
 
-        e_raw, p_raw, p_grouped, p_codes, p_scales = {}, {}, {}, {}, {}
+        e_raw, p_raw, p_codes, p_scales = {}, {}, {}, {}
         row_sum, row_div, row_scale, e_norm = {}, {}, {}, {}
         e_grouped, e_codes, e_scales = {}, {}, {}
         et_ps, xt_ps, x_grouped, z_ps = {}, {}, {}, {}
@@ -165,17 +165,29 @@ def tile_yuyipointupdate_pa_t_kernel(
                     accum_out=row_sum[g][:, k : k + 1],
                 )
 
-        def regroup_nodes(g):
-            p_grouped[g] = pipe2.tile([P, D, PACK], BF16, name="p_grouped", align_bytes=64)
-            nc.vector.tensor_copy(out=p_grouped[g][:], in_=p_raw[g][:].rearrange("p t d -> p d t"))
+        p_grouped = [
+            const.tile([P, P, PACK], BF16, name="p_grouped_0", align_bytes=64),
+            const.tile([P, P, PACK], BF16, name="p_grouped_1", align_bytes=64),
+        ]
 
-        def quantise_nodes(g):
-            p_codes[g] = pipe4.tile([P, D], U32, name="p_codes", align_bytes=64)
-            p_scales[g] = pipe4.tile([P, D], U8, name="p_scales", align_bytes=64)
+        def regroup_nodes(g, dh):
+            nc.gpsimd.tensor_scalar(
+                out=p_grouped[dh][:],
+                in0=p_raw[g][:, :, dh * P : (dh + 1) * P].rearrange("p t d -> p d t"),
+                scalar1=1.0,
+                scalar2=0.0,
+                op0=ALU.mult,
+                op1=ALU.add,
+            )
+
+        def quantise_nodes(g, dh):
+            if dh == 0:
+                p_codes[g] = pipe4.tile([P, D], U32, name="p_codes", align_bytes=64)
+                p_scales[g] = pipe4.tile([P, D], U8, name="p_scales", align_bytes=64)
             nc.vector.quantize_mx(
-                out=p_codes[g][:].bitcast(FP8X4),
-                scales=p_scales[g][:],
-                in_=p_grouped[g][:].rearrange("p d t -> p (d t)"),
+                out=p_codes[g][:, dh * P : (dh + 1) * P].bitcast(FP8X4),
+                scales=p_scales[g][:, dh * P : (dh + 1) * P],
+                in_=p_grouped[dh][:].rearrange("p d t -> p (d t)"),
             )
 
         def clamp_row_sums(g):
@@ -252,7 +264,7 @@ def tile_yuyipointupdate_pa_t_kernel(
         def regroup_x(g, nb):
             if nb == 0:
                 x_grouped[g] = pipe2.tile([P, N, PACK], BF16, name="x_grouped", align_bytes=64)
-            on_scalar = nb % 2 == 0 or (nb == 1 and g % 2 == 1) or g >= B - DRAIN_GRAPHS
+            on_scalar = nb % 2 == 0 or g >= B - DRAIN_GRAPHS
             copy_out = nc.scalar.copy if on_scalar else nc.vector.tensor_copy
             copy_out(
                 out=x_grouped[g][:, nb * P : (nb + 1) * P, :],
@@ -280,6 +292,12 @@ def tile_yuyipointupdate_pa_t_kernel(
             g, q = due(step, ROW_SCALE_AT)
             if g is not None and q == 0:
                 clamp_row_sums(g)
+            g, q = due(step, P_QUANT_AT)
+            if g is not None and q % 2 == 0:
+                quantise_nodes(g, q // 2)
+            g, q = due(step, P_REGROUP_AT)
+            if g is not None and q % 2 == 0:
+                regroup_nodes(g, q // 2)
             g, q = due(step, Z_STATS_AT)
             if g is not None:
                 z_statistics(g, q)
@@ -315,12 +333,6 @@ def tile_yuyipointupdate_pa_t_kernel(
             g, q = due(step, MASK_AT)
             if g is not None:
                 mask_diagonal(g, q)
-            g, q = due(step, P_QUANT_AT)
-            if g is not None and q == 0:
-                quantise_nodes(g)
-            g, q = due(step, P_REGROUP_AT)
-            if g is not None and q == 0:
-                regroup_nodes(g)
             g, q = due(step, ROW_SCALE_AT)
             if g is not None and q == 0:
                 invert_row_sums(g)

@@ -44,6 +44,7 @@ LAST_STEP = QUARTERS * (B - 1) + Z_STATS_AT + (QUARTERS - 1)
 WEIGHTS_STEP = QUARTERS
 FILL_GRAPHS = 3
 DRAIN_GRAPHS = 4
+VECTOR_EVERY = 16
 
 FLOPS = 2 * B * (KINDS * N * N * D + C * C * N)
 
@@ -264,7 +265,7 @@ def tile_yuyipointupdate_pa_t_kernel(
         def regroup_x(g, nb):
             if nb == 0:
                 x_grouped[g] = pipe2.tile([P, N, PACK], BF16, name="x_grouped", align_bytes=64)
-            on_scalar = nb % 2 == 0 or g >= B - DRAIN_GRAPHS
+            on_scalar = nb == 0 or (nb == 2 and g % 2 == 0) or g >= B - DRAIN_GRAPHS
             copy_out = nc.scalar.copy if on_scalar else nc.vector.tensor_copy
             copy_out(
                 out=x_grouped[g][:, nb * P : (nb + 1) * P, :],
@@ -362,30 +363,52 @@ def tile_yuyipointupdate_pa_t_kernel(
             out=bn_shift[:], in0=gb_cols[:, QUARTERS : 2 * QUARTERS], in1=mean_scaled[:]
         )
 
-        for g in range(B):
-            result = pipe3.tile([P, QUARTERS, N], F32)
-            for ob in range(QUARTERS):
-                z_again = z_matmul(g, ob)
-                y = pipe4.tile([P, N], F32)
+        results, ys = {}, {}
+
+        def normalise_z(n):
+            g, ob = divmod(n, QUARTERS)
+            z_again = z_matmul(g, ob)
+            ys[n] = pipe4.tile([P, N], F32, name="y")
+            if n % VECTOR_EVERY == VECTOR_EVERY - 1:
+                nc.vector.tensor_scalar(
+                    out=ys[n][:],
+                    in0=z_again[:],
+                    scalar1=bn_scale[:, ob : ob + 1],
+                    scalar2=bn_shift[:, ob : ob + 1],
+                    op0=ALU.mult,
+                    op1=ALU.add,
+                )
+            else:
                 nc.scalar.activation(
-                    out=y[:],
+                    out=ys[n][:],
                     in_=z_again[:],
                     func=ACT.Identity,
                     scale=bn_scale[:, ob : ob + 1],
                     bias=bn_shift[:, ob : ob + 1],
                 )
-                nc.vector.scalar_tensor_tensor(
-                    out=result[:, ob, :],
-                    in0=y[:],
-                    scalar=NEG_SLOPE,
-                    in1=y[:],
-                    op0=ALU.mult,
-                    op1=ALU.max,
+
+        def leaky_relu(n):
+            g, ob = divmod(n, QUARTERS)
+            if ob == 0:
+                results[g] = pipe3.tile([P, QUARTERS, N], F32, name="result")
+            nc.vector.scalar_tensor_tensor(
+                out=results[g][:, ob, :],
+                in0=ys[n][:],
+                scalar=NEG_SLOPE,
+                in1=ys[n][:],
+                op0=ALU.mult,
+                op1=ALU.max,
+            )
+            stored = 1 if g in (0, B - 1) else 2
+            if (ob + 1) % stored == 0:
+                blocks = slice(ob + 1 - stored, ob + 1)
+                nc.sync.dma_start(
+                    out=out[g].rearrange("(p ob) n -> p ob n", p=P)[:, blocks],
+                    in_=results[g][:, blocks],
                 )
-                stored = 1 if g in (0, B - 1) else 2
-                if (ob + 1) % stored == 0:
-                    blocks = slice(ob + 1 - stored, ob + 1)
-                    nc.sync.dma_start(
-                        out=out[g].rearrange("(p ob) n -> p ob n", p=P)[:, blocks],
-                        in_=result[:, blocks],
-                    )
+
+        normalise_z(0)
+        for n in range(B * QUARTERS):
+            if n + 1 < B * QUARTERS:
+                normalise_z(n + 1)
+            leaky_relu(n)

@@ -37,13 +37,12 @@ E_REGROUP_AT = TRANSPOSE_AT + 1
 E_QUANT_AT = E_REGROUP_AT + 1 + 2
 X_MATMUL_AT = E_QUANT_AT + 2 + 1
 X_REGROUP_AT = X_MATMUL_AT + 1
-X_QUANT_AT = X_REGROUP_AT + (QUARTERS - 1) + 1
-Z_MATMUL_AT = X_QUANT_AT + 1
+X_QUANT_AT = X_REGROUP_AT + 1 + 1
+Z_MATMUL_AT = X_QUANT_AT + 2 + 1
 Z_STATS_AT = Z_MATMUL_AT + 1
 LAST_STEP = QUARTERS * (B - 1) + Z_STATS_AT + (QUARTERS - 1)
 WEIGHTS_STEP = QUARTERS
 FILL_GRAPHS = 3
-DRAIN_GRAPHS = 4
 VECTOR_EVERY = 16
 
 FLOPS = 2 * B * (KINDS * N * N * D + C * C * N)
@@ -154,17 +153,28 @@ def tile_yuyipointupdate_pa_t_kernel(
                 op=ALU.mult,
             )
 
-        def sum_rows(g, r):
-            if r == 0:
-                row_sum[g] = pipe4.tile([P, KINDS * QUARTERS], F32, name="row_sum")
+        def sum_rows_on_scalar(g, r):
             for e in range(KINDS):
                 k = e * QUARTERS + r
+                if e == 1 and r % 2 == 0:
+                    continue
                 nc.scalar.activation(
                     out=e_abs[:, e, r, :],
                     in_=e_raw[g][:, e, r, :],
                     func=ACT.Abs,
                     accum_out=row_sum[g][:, k : k + 1],
                 )
+
+        def sum_rows_on_vector(g, r):
+            if r == 0:
+                row_sum[g] = pipe4.tile([P, KINDS * QUARTERS], F32, name="row_sum")
+            nc.vector.tensor_reduce(
+                out=row_sum[g][:, QUARTERS + r : QUARTERS + r + 1],
+                in_=e_raw[g][:, 1, r, :],
+                axis=mybir.AxisListType.X,
+                op=ALU.add,
+                apply_absolute_value=True,
+            )
 
         p_grouped = [
             const.tile([P, P, PACK], BF16, name="p_grouped_0", align_bytes=64),
@@ -265,18 +275,17 @@ def tile_yuyipointupdate_pa_t_kernel(
         def regroup_x(g, nb):
             if nb == 0:
                 x_grouped[g] = pipe2.tile([P, N, PACK], BF16, name="x_grouped", align_bytes=64)
-            on_scalar = nb == 0 or (nb == 2 and g % 2 == 0) or g >= B - DRAIN_GRAPHS
-            copy_out = nc.scalar.copy if on_scalar else nc.vector.tensor_copy
-            copy_out(
+            nc.scalar.copy(
                 out=x_grouped[g][:, nb * P : (nb + 1) * P, :],
                 in_=xt_ps[g, nb][:].rearrange("p t n -> p n t"),
             )
 
-        def quantise_x(g):
+        def quantise_x(g, half):
+            nodes = slice(half * (N // 2), (half + 1) * (N // 2))
             nc.vector.quantize_mx(
-                out=x_codes[:, g, :].bitcast(FP8X4),
-                scales=x_scales[:, g, :],
-                in_=x_grouped[g][:].rearrange("p n t -> p (n t)"),
+                out=x_codes[:, g, nodes].bitcast(FP8X4),
+                scales=x_scales[:, g, nodes],
+                in_=x_grouped[g][:, nodes, :].rearrange("p n t -> p (n t)"),
             )
 
         def z_first(g, ob):
@@ -302,12 +311,15 @@ def tile_yuyipointupdate_pa_t_kernel(
             g, q = due(step, Z_STATS_AT)
             if g is not None:
                 z_statistics(g, q)
+            g, q = due(step, ABS_AT)
+            if g is not None and q % 2 == 0:
+                sum_rows_on_vector(g, q)
             g, q = due(step, Z_MATMUL_AT)
             if g is not None:
                 z_first(g, q)
             g, q = due(step, X_QUANT_AT)
-            if g is not None and q == 0:
-                quantise_x(g)
+            if g is not None and q % 2 == 0:
+                quantise_x(g, q // 2)
             g, q = due(step, X_REGROUP_AT)
             if g is not None:
                 regroup_x(g, q)
@@ -328,7 +340,7 @@ def tile_yuyipointupdate_pa_t_kernel(
                 normalise_rows(g, q)
             g, q = due(step, ABS_AT)
             if g is not None:
-                sum_rows(g, q)
+                sum_rows_on_scalar(g, q)
             if step == WEIGHTS_STEP:
                 prepare_weights()
             g, q = due(step, MASK_AT)

@@ -19,31 +19,34 @@ D = 256
 C = 2 * D
 KINDS = 2
 QUARTERS = N // P
+DIAGONAL_STEP = N + P
 PSUM_BANKS = 8
 EPS_L1 = 1e-12
 EPS_BN = 1e-5
 NEG_SLOPE = 0.01
 BN_STATS_DIM = 6
 
-LOAD_AT = -2 * QUARTERS
+EDGE_LOAD_AT = -2 * QUARTERS
+NODE_LOAD_AT = -1 * QUARTERS
 MASK_AT = 0
 ABS_AT = MASK_AT + 2
-P_QUANT_AT = 6
-P_REGROUP_AT = P_QUANT_AT - QUARTERS
 ROW_SCALE_AT = ABS_AT + (QUARTERS - 1) + 2
 NORM_AT = ROW_SCALE_AT + 1
-TRANSPOSE_AT = NORM_AT + 1
-E_REGROUP_AT = TRANSPOSE_AT + 1
-E_QUANT_AT = E_REGROUP_AT + 1 + 2
-X_MATMUL_AT = E_QUANT_AT + 2 + 1
+TRANSPOSE_AT = NORM_AT + QUARTERS
+E_REGROUP_AT = TRANSPOSE_AT + 2
+E_QUANT_AT = E_REGROUP_AT + 1 + 1
+P_QUANT_AT = NORM_AT + 2
+P_REGROUP_AT = P_QUANT_AT - QUARTERS
+X_MATMUL_AT = E_QUANT_AT + 2 + 2
 X_REGROUP_AT = X_MATMUL_AT + 1
-X_QUANT_AT = X_REGROUP_AT + 1 + 1
-Z_MATMUL_AT = X_QUANT_AT + 2 + 1
+X_QUANT_AT = X_REGROUP_AT + (QUARTERS - 1) + 1
+Z_MATMUL_AT = X_QUANT_AT + 1
 Z_STATS_AT = Z_MATMUL_AT + 1
 LAST_STEP = QUARTERS * (B - 1) + Z_STATS_AT + (QUARTERS - 1)
-WEIGHTS_STEP = QUARTERS
-FILL_GRAPHS = 3
-VECTOR_EVERY = 16
+WEIGHTS_STEP = 2 * QUARTERS
+FILL_GRAPHS = 1
+DRAIN_GRAPHS = 4
+VECTOR_EVERY = 32
 
 FLOPS = 2 * B * (KINDS * N * N * D + C * C * N)
 
@@ -56,7 +59,6 @@ def tile_yuyipointupdate_pa_t_kernel(
 
     with ExitStack() as ctx:
         const = ctx.enter_context(tc.tile_pool(name="const", bufs=1))
-        pipe2 = ctx.enter_context(tc.tile_pool(name="pipe2", bufs=2))
         pipe3 = ctx.enter_context(tc.tile_pool(name="pipe3", bufs=3))
         pipe4 = ctx.enter_context(tc.tile_pool(name="pipe4", bufs=4))
         psum = ctx.enter_context(tc.psum_pool(name="psum", bufs=PSUM_BANKS))
@@ -129,38 +131,47 @@ def tile_yuyipointupdate_pa_t_kernel(
         e_grouped, e_codes, e_scales = {}, {}, {}
         et_ps, xt_ps, x_grouped, z_ps = {}, {}, {}, {}
 
-        def load(g):
-            e_raw[g] = pipe4.tile([P, KINDS, QUARTERS, N], BF16, name="e_raw")
-            chunk = 1 if g == 0 else QUARTERS
+        def load_edges(g):
+            e_raw[g] = pipe4.tile([P, KINDS, QUARTERS * DIAGONAL_STEP], BF16, name="e_raw")
+            chunk = 1 if g < 2 else QUARTERS
             for r in range(0, QUARTERS, chunk):
                 for e in range(KINDS):
                     nc.sync.dma_start(
-                        out=e_raw[g][:, e, r : r + chunk],
+                        out=e_raw[g][:, e, r * N : (r + chunk) * N].rearrange("p (r m) -> p r m", m=N),
                         in_=edges[e][g].rearrange("(r p) m -> p r m", p=P)[:, r : r + chunk],
                     )
+
+        def load_nodes(g):
             p_raw[g] = pipe3.tile([P, PACK, D], BF16, name="p_raw")
             nc.sync.dma_start(
                 out=p_raw[g][:].rearrange("p (u i) d -> p u (i d)", u=2),
                 in_=point_node[g].rearrange("(u p i) d -> p u (i d)", u=2, i=2),
             )
 
-        def mask_diagonal(g, r):
-            diag_block = e_raw[g][:, :, r, r * P : (r + 1) * P]
+        def row_tile(g, e, r):
+            return e_raw[g][:, e, r * N : (r + 1) * N]
+
+        def mask_diagonals(g, tiles):
+            blocks = e_raw[g][:].rearrange("p e (r x) -> p e r x", x=DIAGONAL_STEP)[:, :, tiles, 0:P]
+            count = tiles.stop - tiles.start
             nc.vector.tensor_tensor(
-                out=diag_block,
-                in0=diag_block,
-                in1=offdiag[:].unsqueeze(1).to_broadcast([P, KINDS, P]),
+                out=blocks,
+                in0=blocks,
+                in1=offdiag[:].unsqueeze(1).unsqueeze(1).to_broadcast([P, KINDS, count, P]),
                 op=ALU.mult,
             )
+
+        def vector_sums_row_tile(g, e, r):
+            return e == 1 and r == 0
 
         def sum_rows_on_scalar(g, r):
             for e in range(KINDS):
                 k = e * QUARTERS + r
-                if e == 1 and r % 2 == 0:
+                if vector_sums_row_tile(g, e, r):
                     continue
                 nc.scalar.activation(
                     out=e_abs[:, e, r, :],
-                    in_=e_raw[g][:, e, r, :],
+                    in_=row_tile(g, e, r),
                     func=ACT.Abs,
                     accum_out=row_sum[g][:, k : k + 1],
                 )
@@ -168,9 +179,11 @@ def tile_yuyipointupdate_pa_t_kernel(
         def sum_rows_on_vector(g, r):
             if r == 0:
                 row_sum[g] = pipe4.tile([P, KINDS * QUARTERS], F32, name="row_sum")
+            if not vector_sums_row_tile(g, 1, r):
+                return
             nc.vector.tensor_reduce(
                 out=row_sum[g][:, QUARTERS + r : QUARTERS + r + 1],
-                in_=e_raw[g][:, 1, r, :],
+                in_=row_tile(g, 1, r),
                 axis=mybir.AxisListType.X,
                 op=ALU.add,
                 apply_absolute_value=True,
@@ -212,12 +225,12 @@ def tile_yuyipointupdate_pa_t_kernel(
         def normalise_rows(g, j):
             e, h = divmod(j, 2)
             if j == 0:
-                e_norm[g] = pipe2.tile([P, KINDS, QUARTERS, N], BF16, name="e_norm")
+                e_norm[g] = pipe3.tile([P, KINDS, QUARTERS, N], BF16, name="e_norm")
             for r in (2 * h, 2 * h + 1):
                 k = e * QUARTERS + r
                 nc.vector.tensor_scalar(
                     out=e_norm[g][:, e, r, :],
-                    in0=e_raw[g][:, e, r, :],
+                    in0=row_tile(g, e, r),
                     scalar1=row_scale[g][:, k : k + 1],
                     scalar2=None,
                     op0=ALU.mult,
@@ -238,7 +251,7 @@ def tile_yuyipointupdate_pa_t_kernel(
         def regroup_edges(g, j):
             e, h = divmod(j, 2)
             if j == 0:
-                e_grouped[g] = pipe2.tile([P, KINDS, N * PACK], BF16, name="e_grouped", align_bytes=64)
+                e_grouped[g] = pipe3.tile([P, KINDS, N * PACK], BF16, name="e_grouped", align_bytes=64)
             e_grouped_words = e_grouped[g][:].bitcast(F32)
             copy_out = nc.vector.tensor_copy if g < FILL_GRAPHS else nc.scalar.copy
             copy_out(
@@ -250,8 +263,8 @@ def tile_yuyipointupdate_pa_t_kernel(
 
         def quantise_edges(g, e):
             if e == 0:
-                e_codes[g] = pipe2.tile([P, KINDS, N], U32, name="e_codes", align_bytes=64)
-                e_scales[g] = pipe2.tile([P, KINDS, N], U8, name="e_scales", align_bytes=64)
+                e_codes[g] = pipe3.tile([P, KINDS, N], U32, name="e_codes", align_bytes=64)
+                e_scales[g] = pipe3.tile([P, KINDS, N], U8, name="e_scales", align_bytes=64)
             nc.vector.quantize_mx(
                 out=e_codes[g][:, e, :].bitcast(FP8X4),
                 scales=e_scales[g][:, e, :],
@@ -274,18 +287,19 @@ def tile_yuyipointupdate_pa_t_kernel(
 
         def regroup_x(g, nb):
             if nb == 0:
-                x_grouped[g] = pipe2.tile([P, N, PACK], BF16, name="x_grouped", align_bytes=64)
-            nc.scalar.copy(
+                x_grouped[g] = pipe3.tile([P, N, PACK], BF16, name="x_grouped", align_bytes=64)
+            on_scalar = nb % 2 == 0 or g >= B - DRAIN_GRAPHS
+            copy_out = nc.scalar.copy if on_scalar else nc.vector.tensor_copy
+            copy_out(
                 out=x_grouped[g][:, nb * P : (nb + 1) * P, :],
                 in_=xt_ps[g, nb][:].rearrange("p t n -> p n t"),
             )
 
-        def quantise_x(g, half):
-            nodes = slice(half * (N // 2), (half + 1) * (N // 2))
+        def quantise_x(g):
             nc.vector.quantize_mx(
-                out=x_codes[:, g, nodes].bitcast(FP8X4),
-                scales=x_scales[:, g, nodes],
-                in_=x_grouped[g][:, nodes, :].rearrange("p n t -> p (n t)"),
+                out=x_codes[:, g, :].bitcast(FP8X4),
+                scales=x_scales[:, g, :],
+                in_=x_grouped[g][:].rearrange("p n t -> p (n t)"),
             )
 
         def z_first(g, ob):
@@ -298,7 +312,7 @@ def tile_yuyipointupdate_pa_t_kernel(
             g, q = divmod(step - first_step, QUARTERS)
             return (g, q) if 0 <= g < B else (None, q)
 
-        for step in range(LOAD_AT, LAST_STEP + 1):
+        for step in range(EDGE_LOAD_AT, LAST_STEP + 1):
             g, q = due(step, ROW_SCALE_AT)
             if g is not None and q == 0:
                 clamp_row_sums(g)
@@ -312,14 +326,14 @@ def tile_yuyipointupdate_pa_t_kernel(
             if g is not None:
                 z_statistics(g, q)
             g, q = due(step, ABS_AT)
-            if g is not None and q % 2 == 0:
+            if g is not None and q == 0:
                 sum_rows_on_vector(g, q)
             g, q = due(step, Z_MATMUL_AT)
             if g is not None:
                 z_first(g, q)
             g, q = due(step, X_QUANT_AT)
-            if g is not None and q % 2 == 0:
-                quantise_x(g, q // 2)
+            if g is not None and q == 0:
+                quantise_x(g)
             g, q = due(step, X_REGROUP_AT)
             if g is not None:
                 regroup_x(g, q)
@@ -344,14 +358,19 @@ def tile_yuyipointupdate_pa_t_kernel(
             if step == WEIGHTS_STEP:
                 prepare_weights()
             g, q = due(step, MASK_AT)
-            if g is not None:
-                mask_diagonal(g, q)
+            if g == 0:
+                mask_diagonals(g, slice(q, q + 1))
+            elif g is not None and q == 0:
+                mask_diagonals(g, slice(0, QUARTERS))
             g, q = due(step, ROW_SCALE_AT)
             if g is not None and q == 0:
                 invert_row_sums(g)
-            g, q = due(step, LOAD_AT)
+            g, q = due(step, EDGE_LOAD_AT)
             if g is not None and q == 0:
-                load(g)
+                load_edges(g)
+            g, q = due(step, NODE_LOAD_AT)
+            if g is not None and q == 0:
+                load_nodes(g)
                 if g == 0:
                     load_weights()
 
@@ -360,16 +379,16 @@ def tile_yuyipointupdate_pa_t_kernel(
             nc.vector.bn_aggr(
                 out=mean_var[:, ob, :], in_=stats[:, ob, :, :].rearrange("p g s -> p (g s)")
             )
-        var_eps = const.tile([P, QUARTERS], F32)
-        nc.vector.tensor_scalar_add(out=var_eps[:], in0=mean_var[:, :, 1], scalar1=EPS_BN)
         std = const.tile([P, QUARTERS], F32)
-        nc.scalar.sqrt(out=std[:], in_=var_eps[:])
+        nc.scalar.activation(out=std[:], in_=mean_var[:, :, 1], func=ACT.Sqrt, bias=EPS_BN, scale=1.0)
+        gain_mean = const.tile([P, QUARTERS], F32)
+        nc.vector.tensor_mul(out=gain_mean[:], in0=gb_cols[:, 0:QUARTERS], in1=mean_var[:, :, 0])
         inv_std = const.tile([P, QUARTERS], F32)
         nc.vector.reciprocal(out=inv_std[:], in_=std[:])
+        mean_scaled = const.tile([P, QUARTERS], F32)
+        nc.vector.tensor_mul(out=mean_scaled[:], in0=gain_mean[:], in1=inv_std[:])
         bn_scale = const.tile([P, QUARTERS], F32)
         nc.vector.tensor_mul(out=bn_scale[:], in0=gb_cols[:, 0:QUARTERS], in1=inv_std[:])
-        mean_scaled = const.tile([P, QUARTERS], F32)
-        nc.vector.tensor_mul(out=mean_scaled[:], in0=mean_var[:, :, 0], in1=bn_scale[:])
         bn_shift = const.tile([P, QUARTERS], F32)
         nc.vector.tensor_sub(
             out=bn_shift[:], in0=gb_cols[:, QUARTERS : 2 * QUARTERS], in1=mean_scaled[:]
@@ -377,47 +396,53 @@ def tile_yuyipointupdate_pa_t_kernel(
 
         results, ys = {}, {}
 
+        def column_parts(n):
+            parts = 2 if n == B * QUARTERS - 1 else 1
+            return [slice(i * (N // parts), (i + 1) * (N // parts)) for i in range(parts)]
+
         def normalise_z(n):
             g, ob = divmod(n, QUARTERS)
             z_again = z_matmul(g, ob)
             ys[n] = pipe4.tile([P, N], F32, name="y")
-            if n % VECTOR_EVERY == VECTOR_EVERY - 1:
-                nc.vector.tensor_scalar(
-                    out=ys[n][:],
-                    in0=z_again[:],
-                    scalar1=bn_scale[:, ob : ob + 1],
-                    scalar2=bn_shift[:, ob : ob + 1],
-                    op0=ALU.mult,
-                    op1=ALU.add,
-                )
-            else:
-                nc.scalar.activation(
-                    out=ys[n][:],
-                    in_=z_again[:],
-                    func=ACT.Identity,
-                    scale=bn_scale[:, ob : ob + 1],
-                    bias=bn_shift[:, ob : ob + 1],
-                )
+            for cols in column_parts(n):
+                if n % VECTOR_EVERY == VECTOR_EVERY // 2:
+                    nc.vector.tensor_scalar(
+                        out=ys[n][:, cols],
+                        in0=z_again[:, cols],
+                        scalar1=bn_scale[:, ob : ob + 1],
+                        scalar2=bn_shift[:, ob : ob + 1],
+                        op0=ALU.mult,
+                        op1=ALU.add,
+                    )
+                else:
+                    nc.scalar.activation(
+                        out=ys[n][:, cols],
+                        in_=z_again[:, cols],
+                        func=ACT.Identity,
+                        scale=bn_scale[:, ob : ob + 1],
+                        bias=bn_shift[:, ob : ob + 1],
+                    )
 
         def leaky_relu(n):
             g, ob = divmod(n, QUARTERS)
             if ob == 0:
                 results[g] = pipe3.tile([P, QUARTERS, N], F32, name="result")
-            nc.vector.scalar_tensor_tensor(
-                out=results[g][:, ob, :],
-                in0=ys[n][:],
-                scalar=NEG_SLOPE,
-                in1=ys[n][:],
-                op0=ALU.mult,
-                op1=ALU.max,
-            )
             stored = 1 if g in (0, B - 1) else 2
-            if (ob + 1) % stored == 0:
-                blocks = slice(ob + 1 - stored, ob + 1)
-                nc.sync.dma_start(
-                    out=out[g].rearrange("(p ob) n -> p ob n", p=P)[:, blocks],
-                    in_=results[g][:, blocks],
+            blocks = slice(ob + 1 - stored, ob + 1)
+            for cols in column_parts(n):
+                nc.vector.scalar_tensor_tensor(
+                    out=results[g][:, ob, cols],
+                    in0=ys[n][:, cols],
+                    scalar=NEG_SLOPE,
+                    in1=ys[n][:, cols],
+                    op0=ALU.mult,
+                    op1=ALU.max,
                 )
+                if (ob + 1) % stored == 0:
+                    nc.sync.dma_start(
+                        out=out[g].rearrange("(p ob) n -> p ob n", p=P)[:, blocks, cols],
+                        in_=results[g][:, blocks, cols],
+                    )
 
         normalise_z(0)
         for n in range(B * QUARTERS):

@@ -32,12 +32,12 @@ MASK_AT = 0
 ABS_AT = MASK_AT + 2
 ROW_SCALE_AT = ABS_AT + (QUARTERS - 1) + 2
 NORM_AT = ROW_SCALE_AT + 1
-TRANSPOSE_AT = NORM_AT + QUARTERS
-E_REGROUP_AT = TRANSPOSE_AT + 2
-E_QUANT_AT = E_REGROUP_AT + 1 + 1
-P_QUANT_AT = NORM_AT + 2
+TRANSPOSE_AT = NORM_AT + 2
+E_REGROUP_AT = TRANSPOSE_AT + 1
+E_QUANT_AT = E_REGROUP_AT + 1 + 2
+P_QUANT_AT = NORM_AT + QUARTERS
 P_REGROUP_AT = P_QUANT_AT - QUARTERS
-X_MATMUL_AT = E_QUANT_AT + 2 + 2
+X_MATMUL_AT = E_QUANT_AT + 2 + 1
 X_REGROUP_AT = X_MATMUL_AT + 1
 X_QUANT_AT = X_REGROUP_AT + (QUARTERS - 1) + 1
 Z_MATMUL_AT = X_QUANT_AT + 1
@@ -46,7 +46,6 @@ LAST_STEP = QUARTERS * (B - 1) + Z_STATS_AT + (QUARTERS - 1)
 WEIGHTS_STEP = 2 * QUARTERS
 FILL_GRAPHS = 1
 DRAIN_GRAPHS = 4
-VECTOR_EVERY = 32
 
 FLOPS = 2 * B * (KINDS * N * N * D + C * C * N)
 
@@ -162,7 +161,7 @@ def tile_yuyipointupdate_pa_t_kernel(
             )
 
         def vector_sums_row_tile(g, e, r):
-            return e == 1 and r == 0
+            return e == 1 and (r == 0 or (r == 2 and g % 2 == 0))
 
         def sum_rows_on_scalar(g, r):
             for e in range(KINDS):
@@ -216,7 +215,7 @@ def tile_yuyipointupdate_pa_t_kernel(
 
         def clamp_row_sums(g):
             row_div[g] = pipe4.tile([P, KINDS * QUARTERS], F32, name="row_div")
-            nc.vector.tensor_scalar_max(out=row_div[g][:], in0=row_sum[g][:], scalar1=EPS_L1)
+            nc.gpsimd.tensor_scalar_max(out=row_div[g][:], in0=row_sum[g][:], scalar1=EPS_L1)
 
         def invert_row_sums(g):
             row_scale[g] = pipe4.tile([P, KINDS * QUARTERS], F32, name="row_scale")
@@ -288,7 +287,7 @@ def tile_yuyipointupdate_pa_t_kernel(
         def regroup_x(g, nb):
             if nb == 0:
                 x_grouped[g] = pipe3.tile([P, N, PACK], BF16, name="x_grouped", align_bytes=64)
-            on_scalar = nb % 2 == 0 or g >= B - DRAIN_GRAPHS
+            on_scalar = nb != 2 or g >= B - DRAIN_GRAPHS
             copy_out = nc.scalar.copy if on_scalar else nc.vector.tensor_copy
             copy_out(
                 out=x_grouped[g][:, nb * P : (nb + 1) * P, :],
@@ -326,7 +325,7 @@ def tile_yuyipointupdate_pa_t_kernel(
             if g is not None:
                 z_statistics(g, q)
             g, q = due(step, ABS_AT)
-            if g is not None and q == 0:
+            if g is not None:
                 sum_rows_on_vector(g, q)
             g, q = due(step, Z_MATMUL_AT)
             if g is not None:
@@ -405,23 +404,13 @@ def tile_yuyipointupdate_pa_t_kernel(
             z_again = z_matmul(g, ob)
             ys[n] = pipe4.tile([P, N], F32, name="y")
             for cols in column_parts(n):
-                if n % VECTOR_EVERY == VECTOR_EVERY // 2:
-                    nc.vector.tensor_scalar(
-                        out=ys[n][:, cols],
-                        in0=z_again[:, cols],
-                        scalar1=bn_scale[:, ob : ob + 1],
-                        scalar2=bn_shift[:, ob : ob + 1],
-                        op0=ALU.mult,
-                        op1=ALU.add,
-                    )
-                else:
-                    nc.scalar.activation(
-                        out=ys[n][:, cols],
-                        in_=z_again[:, cols],
-                        func=ACT.Identity,
-                        scale=bn_scale[:, ob : ob + 1],
-                        bias=bn_shift[:, ob : ob + 1],
-                    )
+                nc.scalar.activation(
+                    out=ys[n][:, cols],
+                    in_=z_again[:, cols],
+                    func=ACT.Identity,
+                    scale=bn_scale[:, ob : ob + 1],
+                    bias=bn_shift[:, ob : ob + 1],
+                )
 
         def leaky_relu(n):
             g, ob = divmod(n, QUARTERS)
@@ -444,8 +433,6 @@ def tile_yuyipointupdate_pa_t_kernel(
                         in_=results[g][:, blocks, cols],
                     )
 
-        normalise_z(0)
         for n in range(B * QUARTERS):
-            if n + 1 < B * QUARTERS:
-                normalise_z(n + 1)
+            normalise_z(n)
             leaky_relu(n)

@@ -46,6 +46,9 @@ LAST_STEP = QUARTERS * (B - 1) + Z_STATS_AT + (QUARTERS - 1)
 WEIGHTS_STEP = 2 * QUARTERS
 FILL_GRAPHS = 1
 DRAIN_GRAPHS = 4
+HEAD_BLOCKS = [0]
+OTHER_BLOCKS = [1, 2, 3]
+HEAD_GRAPHS = 4
 
 FLOPS = 2 * B * (KINDS * N * N * D + C * C * N)
 
@@ -58,8 +61,10 @@ def tile_yuyipointupdate_pa_t_kernel(
 
     with ExitStack() as ctx:
         const = ctx.enter_context(tc.tile_pool(name="const", bufs=1))
+        pipe2 = ctx.enter_context(tc.tile_pool(name="pipe2", bufs=2))
         pipe3 = ctx.enter_context(tc.tile_pool(name="pipe3", bufs=3))
         pipe4 = ctx.enter_context(tc.tile_pool(name="pipe4", bufs=4))
+        pipe6 = ctx.enter_context(tc.tile_pool(name="pipe6", bufs=6))
         psum = ctx.enter_context(tc.psum_pool(name="psum", bufs=PSUM_BANKS))
         ctx.enter_context(tc.manual_schedule())
 
@@ -250,7 +255,7 @@ def tile_yuyipointupdate_pa_t_kernel(
         def regroup_edges(g, j):
             e, h = divmod(j, 2)
             if j == 0:
-                e_grouped[g] = pipe3.tile([P, KINDS, N * PACK], BF16, name="e_grouped", align_bytes=64)
+                e_grouped[g] = pipe2.tile([P, KINDS, N * PACK], BF16, name="e_grouped", align_bytes=64)
             e_grouped_words = e_grouped[g][:].bitcast(F32)
             copy_out = nc.vector.tensor_copy if g < FILL_GRAPHS else nc.scalar.copy
             copy_out(
@@ -262,8 +267,8 @@ def tile_yuyipointupdate_pa_t_kernel(
 
         def quantise_edges(g, e):
             if e == 0:
-                e_codes[g] = pipe3.tile([P, KINDS, N], U32, name="e_codes", align_bytes=64)
-                e_scales[g] = pipe3.tile([P, KINDS, N], U8, name="e_scales", align_bytes=64)
+                e_codes[g] = pipe2.tile([P, KINDS, N], U32, name="e_codes", align_bytes=64)
+                e_scales[g] = pipe2.tile([P, KINDS, N], U8, name="e_scales", align_bytes=64)
             nc.vector.quantize_mx(
                 out=e_codes[g][:, e, :].bitcast(FP8X4),
                 scales=e_scales[g][:, e, :],
@@ -286,7 +291,7 @@ def tile_yuyipointupdate_pa_t_kernel(
 
         def regroup_x(g, nb):
             if nb == 0:
-                x_grouped[g] = pipe3.tile([P, N, PACK], BF16, name="x_grouped", align_bytes=64)
+                x_grouped[g] = pipe2.tile([P, N, PACK], BF16, name="x_grouped", align_bytes=64)
             on_scalar = nb != 2 or g >= B - DRAIN_GRAPHS
             copy_out = nc.scalar.copy if on_scalar else nc.vector.tensor_copy
             copy_out(
@@ -307,6 +312,45 @@ def tile_yuyipointupdate_pa_t_kernel(
         def z_statistics(g, ob):
             nc.vector.bn_stats(out=stats[:, ob, g, :], in_=z_ps[g, ob][:])
 
+        bn_scale, bn_shift, bn_parts = {}, {}, {}
+
+        def start_batch_norm(obs):
+            count = len(obs)
+            mean_var = const.tile([P, count, 2], F32, name="mean_var_%d" % count)
+            for i, ob in enumerate(obs):
+                nc.vector.bn_aggr(
+                    out=mean_var[:, i, :], in_=stats[:, ob, :, :].rearrange("p g s -> p (g s)")
+                )
+            std = const.tile([P, count], F32, name="std_%d" % count)
+            nc.scalar.activation(
+                out=std[:], in_=mean_var[:, :, 1], func=ACT.Sqrt, bias=EPS_BN, scale=1.0
+            )
+            gain_mean = const.tile([P, count], F32, name="gain_mean_%d" % count)
+            nc.vector.tensor_mul(
+                out=gain_mean[:], in0=gb_cols[:, obs[0] : obs[0] + count], in1=mean_var[:, :, 0]
+            )
+            bn_parts[count] = (std, gain_mean)
+
+        def finish_batch_norm(obs):
+            count = len(obs)
+            std, gain_mean = bn_parts[count]
+            inv_std = const.tile([P, count], F32, name="inv_std_%d" % count)
+            nc.vector.reciprocal(out=inv_std[:], in_=std[:])
+            mean_scaled = const.tile([P, count], F32, name="mean_scaled_%d" % count)
+            nc.vector.tensor_mul(out=mean_scaled[:], in0=gain_mean[:], in1=inv_std[:])
+            scale = const.tile([P, count], F32, name="bn_scale_%d" % count)
+            nc.vector.tensor_mul(
+                out=scale[:], in0=gb_cols[:, obs[0] : obs[0] + count], in1=inv_std[:]
+            )
+            shift = const.tile([P, count], F32, name="bn_shift_%d" % count)
+            first_b = QUARTERS + obs[0]
+            nc.vector.tensor_sub(
+                out=shift[:], in0=gb_cols[:, first_b : first_b + count], in1=mean_scaled[:]
+            )
+            for i, ob in enumerate(obs):
+                bn_scale[ob] = scale[:, i : i + 1]
+                bn_shift[ob] = shift[:, i : i + 1]
+
         def due(step, first_step):
             g, q = divmod(step - first_step, QUARTERS)
             return (g, q) if 0 <= g < B else (None, q)
@@ -324,6 +368,14 @@ def tile_yuyipointupdate_pa_t_kernel(
             g, q = due(step, Z_STATS_AT)
             if g is not None:
                 z_statistics(g, q)
+            if g == B - 1:
+                if q == 0:
+                    start_batch_norm(HEAD_BLOCKS)
+                elif q == 1:
+                    finish_batch_norm(HEAD_BLOCKS)
+                elif q == QUARTERS - 1:
+                    start_batch_norm(OTHER_BLOCKS)
+                    finish_batch_norm(OTHER_BLOCKS)
             g, q = due(step, ABS_AT)
             if g is not None:
                 sum_rows_on_vector(g, q)
@@ -373,66 +425,45 @@ def tile_yuyipointupdate_pa_t_kernel(
                 if g == 0:
                     load_weights()
 
-        mean_var = const.tile([P, QUARTERS, 2], F32)
-        for ob in range(QUARTERS):
-            nc.vector.bn_aggr(
-                out=mean_var[:, ob, :], in_=stats[:, ob, :, :].rearrange("p g s -> p (g s)")
-            )
-        std = const.tile([P, QUARTERS], F32)
-        nc.scalar.activation(out=std[:], in_=mean_var[:, :, 1], func=ACT.Sqrt, bias=EPS_BN, scale=1.0)
-        gain_mean = const.tile([P, QUARTERS], F32)
-        nc.vector.tensor_mul(out=gain_mean[:], in0=gb_cols[:, 0:QUARTERS], in1=mean_var[:, :, 0])
-        inv_std = const.tile([P, QUARTERS], F32)
-        nc.vector.reciprocal(out=inv_std[:], in_=std[:])
-        mean_scaled = const.tile([P, QUARTERS], F32)
-        nc.vector.tensor_mul(out=mean_scaled[:], in0=gain_mean[:], in1=inv_std[:])
-        bn_scale = const.tile([P, QUARTERS], F32)
-        nc.vector.tensor_mul(out=bn_scale[:], in0=gb_cols[:, 0:QUARTERS], in1=inv_std[:])
-        bn_shift = const.tile([P, QUARTERS], F32)
-        nc.vector.tensor_sub(
-            out=bn_shift[:], in0=gb_cols[:, QUARTERS : 2 * QUARTERS], in1=mean_scaled[:]
-        )
+        ys = {}
 
-        results, ys = {}, {}
-
-        def column_parts(n):
-            parts = 2 if n == B * QUARTERS - 1 else 1
-            return [slice(i * (N // parts), (i + 1) * (N // parts)) for i in range(parts)]
-
-        def normalise_z(n):
-            g, ob = divmod(n, QUARTERS)
-            z_again = z_matmul(g, ob)
-            ys[n] = pipe4.tile([P, N], F32, name="y")
-            for cols in column_parts(n):
-                nc.scalar.activation(
-                    out=ys[n][:, cols],
-                    in_=z_again[:, cols],
-                    func=ACT.Identity,
-                    scale=bn_scale[:, ob : ob + 1],
-                    bias=bn_shift[:, ob : ob + 1],
-                )
-
-        def leaky_relu(n):
-            g, ob = divmod(n, QUARTERS)
-            if ob == 0:
-                results[g] = pipe3.tile([P, QUARTERS, N], F32, name="result")
-            stored = 1 if g in (0, B - 1) else 2
-            blocks = slice(ob + 1 - stored, ob + 1)
-            for cols in column_parts(n):
+        def second_pass(g, blocks, parts=1):
+            if g not in ys:
+                ys[g] = pipe6.tile([P, QUARTERS, N], F32, name="y")
+            y = ys[g]
+            z_banks = [z_matmul(g, ob) for ob in blocks]
+            run = slice(blocks[0], blocks[-1] + 1)
+            for i in range(parts):
+                cols = slice(i * (N // parts), (i + 1) * (N // parts))
+                for z_again, ob in zip(z_banks, blocks):
+                    nc.scalar.activation(
+                        out=y[:, ob, cols],
+                        in_=z_again[:, cols],
+                        func=ACT.Identity,
+                        scale=bn_scale[ob],
+                        bias=bn_shift[ob],
+                    )
                 nc.vector.scalar_tensor_tensor(
-                    out=results[g][:, ob, cols],
-                    in0=ys[n][:, cols],
+                    out=y[:, run, cols],
+                    in0=y[:, run, cols],
                     scalar=NEG_SLOPE,
-                    in1=ys[n][:, cols],
+                    in1=y[:, run, cols],
                     op0=ALU.mult,
                     op1=ALU.max,
                 )
-                if (ob + 1) % stored == 0:
-                    nc.sync.dma_start(
-                        out=out[g].rearrange("(p ob) n -> p ob n", p=P)[:, blocks, cols],
-                        in_=results[g][:, blocks, cols],
-                    )
+                nc.sync.dma_start(
+                    out=out[g].rearrange("(p ob) n -> p ob n", p=P)[:, run, cols],
+                    in_=y[:, run, cols],
+                )
 
-        for n in range(B * QUARTERS):
-            normalise_z(n)
-            leaky_relu(n)
+        for g in range(HEAD_GRAPHS):
+            second_pass(g, HEAD_BLOCKS)
+        for g in range(HEAD_GRAPHS):
+            second_pass(g, [1])
+            second_pass(g, [2, 3])
+        for g in range(HEAD_GRAPHS, B - 1):
+            second_pass(g, [0, 1])
+            second_pass(g, [2, 3])
+        for ob in range(QUARTERS - 1):
+            second_pass(B - 1, [ob])
+        second_pass(B - 1, [QUARTERS - 1], parts=2)

from contextlib import ExitStack

import concourse.mybir as mybir
from concourse.masks import make_identity

F32 = mybir.dt.float32
BF16 = mybir.dt.bfloat16
U32 = mybir.dt.uint32
U8 = mybir.dt.uint8
FP8X4 = mybir.dt.float8_e4m3fn_x4
ALU = mybir.AluOpType
ACT = mybir.ActivationFunctionType

P = 128
PACK = 4
B = 16
N = 512
D = 256
C = 2 * D
KINDS = 2
QUARTERS = N // P
DIAGONAL_STEP = N + P
PSUM_BANKS = 8
EPS_L1 = 1e-12
EPS_BN = 1e-5
NEG_SLOPE = 0.01
BN_STATS_DIM = 6

EDGE_LOAD_AT = -2 * QUARTERS
NODE_LOAD_AT = -1 * QUARTERS
MASK_AT = 0
ABS_AT = MASK_AT + 2
ROW_SCALE_AT = ABS_AT + (QUARTERS - 1) + 2
NORM_AT = ROW_SCALE_AT + 1
TRANSPOSE_AT = NORM_AT + 2
E_REGROUP_AT = TRANSPOSE_AT + 1
E_QUANT_AT = E_REGROUP_AT + 1 + 2
P_QUANT_AT = NORM_AT + QUARTERS
P_REGROUP_AT = P_QUANT_AT - QUARTERS
X_MATMUL_AT = E_QUANT_AT + 2 + 1
X_REGROUP_AT = X_MATMUL_AT + 1
X_QUANT_AT = X_REGROUP_AT + (QUARTERS - 1) + 1
Z_MATMUL_AT = X_QUANT_AT + 1
Z_STATS_AT = Z_MATMUL_AT + 1
LAST_STEP = QUARTERS * (B - 1) + Z_STATS_AT + (QUARTERS - 1)
WEIGHTS_STEP = 2 * QUARTERS
FILL_GRAPHS = 1
DRAIN_GRAPHS = 4
HEAD_BLOCKS = [0]
OTHER_BLOCKS = [1, 2, 3]
HEAD_GRAPHS = 4

FLOPS = 2 * B * (KINDS * N * N * D + C * C * N)


def tile_yuyipointupdate_pa_t_kernel(
    tc, distribution_edge, instance_edge, point_node, W1, g1, b1, out
):
    nc = tc.nc
    edges = (distribution_edge, instance_edge)

    with ExitStack() as ctx:
        const = ctx.enter_context(tc.tile_pool(name="const", bufs=1))
        pipe2 = ctx.enter_context(tc.tile_pool(name="pipe2", bufs=2))
        pipe3 = ctx.enter_context(tc.tile_pool(name="pipe3", bufs=3))
        pipe4 = ctx.enter_context(tc.tile_pool(name="pipe4", bufs=4))
        pipe6 = ctx.enter_context(tc.tile_pool(name="pipe6", bufs=6))
        psum = ctx.enter_context(tc.psum_pool(name="psum", bufs=PSUM_BANKS))
        ctx.enter_context(tc.manual_schedule())

        ident_f32 = const.tile([P, P], F32)
        make_identity(nc, ident_f32[:])
        ident_bf16 = const.tile([P, P], BF16)
        nc.vector.tensor_copy(out=ident_bf16[:], in_=ident_f32[:])
        offdiag = const.tile([P, P], BF16)
        nc.vector.tensor_scalar(
            out=offdiag[:], in0=ident_f32[:], scalar1=-1.0, scalar2=1.0, op0=ALU.mult, op1=ALU.add
        )
        one = const.tile([P, 1], F32)
        nc.vector.memset(one[:], 1.0)
        sqrt_of_one = const.tile([P, 1], F32)
        nc.scalar.sqrt(out=sqrt_of_one[:], in_=one[:])

        w_raw = const.tile([P, QUARTERS, C], BF16)
        w_grouped = const.tile([P, QUARTERS, P, PACK], BF16, align_bytes=64)
        w_codes = const.tile([P, C], U32, align_bytes=64)
        w_scales = const.tile([P, C], U8, align_bytes=64)
        gb_raw = const.tile([P, 2, 16], BF16)
        gb_cols = const.tile([P, 2 * QUARTERS], F32)

        def load_weights():
            nc.sync.dma_start(out=w_raw[:], in_=W1.rearrange("(p ob) c -> p ob c", p=P))
            nc.sync.dma_start(out=gb_raw[:, 0, 0:QUARTERS], in_=g1.rearrange("(p ob) -> p ob", p=P))
            nc.sync.dma_start(out=gb_raw[:, 1, 0:QUARTERS], in_=b1.rearrange("(p ob) -> p ob", p=P))

        def prepare_weights():
            for ob in range(QUARTERS):
                wt_ps = psum.tile([P, PACK, P], BF16, tag="bank")
                for t in range(PACK):
                    nc.tensor.transpose(
                        out=wt_ps[:, t, :],
                        in_=w_raw[:, ob, t * P : (t + 1) * P],
                        identity=ident_bf16[:],
                    )
                nc.vector.tensor_copy(out=w_grouped[:, ob], in_=wt_ps[:].rearrange("p t o -> p o t"))
            nc.vector.tensor_copy(
                out=gb_cols[:].rearrange("p (k ob) -> p k ob", k=2), in_=gb_raw[:, :, 0:QUARTERS]
            )
            nc.vector.quantize_mx(
                out=w_codes[:].bitcast(FP8X4),
                scales=w_scales[:],
                in_=w_grouped[:].rearrange("p ob o t -> p (ob o t)"),
            )

        x_codes = const.tile([P, B, N], U32, align_bytes=64)
        x_scales = const.tile([P, B, N], U8, align_bytes=64)
        stats = const.tile([P, QUARTERS, B, BN_STATS_DIM], F32)
        e_abs = const.tile([P, KINDS, QUARTERS, N], BF16)

        def z_matmul(g, ob):
            z_bank = psum.tile([P, N], F32, tag="bank")
            nc.tensor.matmul_mx(
                out=z_bank[:],
                lhsT=w_codes[:, ob * P : (ob + 1) * P].bitcast(FP8X4),
                lhsT_scale=w_scales[:, ob * P : (ob + 1) * P],
                rhs=x_codes[:, g, :].bitcast(FP8X4),
                rhs_scale=x_scales[:, g, :],
                start=True,
                stop=True,
            )
            return z_bank

        e_raw, p_raw, p_codes, p_scales = {}, {}, {}, {}
        row_sum, row_div, row_scale, e_norm = {}, {}, {}, {}
        e_grouped, e_codes, e_scales = {}, {}, {}
        et_ps, xt_ps, x_grouped, z_ps = {}, {}, {}, {}

        def load_edges(g):
            e_raw[g] = pipe4.tile([P, KINDS, QUARTERS * DIAGONAL_STEP], BF16, name="e_raw")
            chunk = 1 if g < 2 else QUARTERS
            for r in range(0, QUARTERS, chunk):
                for e in range(KINDS):
                    nc.sync.dma_start(
                        out=e_raw[g][:, e, r * N : (r + chunk) * N].rearrange("p (r m) -> p r m", m=N),
                        in_=edges[e][g].rearrange("(r p) m -> p r m", p=P)[:, r : r + chunk],
                    )

        def load_nodes(g):
            p_raw[g] = pipe3.tile([P, PACK, D], BF16, name="p_raw")
            nc.sync.dma_start(
                out=p_raw[g][:].rearrange("p (u i) d -> p u (i d)", u=2),
                in_=point_node[g].rearrange("(u p i) d -> p u (i d)", u=2, i=2),
            )

        def row_tile(g, e, r):
            return e_raw[g][:, e, r * N : (r + 1) * N]

        def mask_diagonals(g, tiles):
            blocks = e_raw[g][:].rearrange("p e (r x) -> p e r x", x=DIAGONAL_STEP)[:, :, tiles, 0:P]
            count = tiles.stop - tiles.start
            nc.vector.tensor_tensor(
                out=blocks,
                in0=blocks,
                in1=offdiag[:].unsqueeze(1).unsqueeze(1).to_broadcast([P, KINDS, count, P]),
                op=ALU.mult,
            )

        def vector_sums_row_tile(g, e, r):
            return e == 1 and (r == 0 or (r == 2 and g % 2 == 0))

        def sum_rows_on_scalar(g, r):
            for e in range(KINDS):
                k = e * QUARTERS + r
                if vector_sums_row_tile(g, e, r):
                    continue
                nc.scalar.activation(
                    out=e_abs[:, e, r, :],
                    in_=row_tile(g, e, r),
                    func=ACT.Abs,
                    accum_out=row_sum[g][:, k : k + 1],
                )

        def sum_rows_on_vector(g, r):
            if r == 0:
                row_sum[g] = pipe4.tile([P, KINDS * QUARTERS], F32, name="row_sum")
            if not vector_sums_row_tile(g, 1, r):
                return
            nc.vector.tensor_reduce(
                out=row_sum[g][:, QUARTERS + r : QUARTERS + r + 1],
                in_=row_tile(g, 1, r),
                axis=mybir.AxisListType.X,
                op=ALU.add,
                apply_absolute_value=True,
            )

        p_grouped = [
            const.tile([P, P, PACK], BF16, name="p_grouped_0", align_bytes=64),
            const.tile([P, P, PACK], BF16, name="p_grouped_1", align_bytes=64),
        ]

        def regroup_nodes(g, dh):
            nc.gpsimd.tensor_scalar(
                out=p_grouped[dh][:],
                in0=p_raw[g][:, :, dh * P : (dh + 1) * P].rearrange("p t d -> p d t"),
                scalar1=1.0,
                scalar2=0.0,
                op0=ALU.mult,
                op1=ALU.add,
            )

        def quantise_nodes(g, dh):
            if dh == 0:
                p_codes[g] = pipe4.tile([P, D], U32, name="p_codes", align_bytes=64)
                p_scales[g] = pipe4.tile([P, D], U8, name="p_scales", align_bytes=64)
            nc.vector.quantize_mx(
                out=p_codes[g][:, dh * P : (dh + 1) * P].bitcast(FP8X4),
                scales=p_scales[g][:, dh * P : (dh + 1) * P],
                in_=p_grouped[dh][:].rearrange("p d t -> p (d t)"),
            )

        def clamp_row_sums(g):
            row_div[g] = pipe4.tile([P, KINDS * QUARTERS], F32, name="row_div")
            nc.gpsimd.tensor_scalar_max(out=row_div[g][:], in0=row_sum[g][:], scalar1=EPS_L1)

        def invert_row_sums(g):
            row_scale[g] = pipe4.tile([P, KINDS * QUARTERS], F32, name="row_scale")
            nc.vector.reciprocal(out=row_scale[g][:], in_=row_div[g][:])

        def normalise_rows(g, j):
            e, h = divmod(j, 2)
            if j == 0:
                e_norm[g] = pipe3.tile([P, KINDS, QUARTERS, N], BF16, name="e_norm")
            for r in (2 * h, 2 * h + 1):
                k = e * QUARTERS + r
                nc.vector.tensor_scalar(
                    out=e_norm[g][:, e, r, :],
                    in0=row_tile(g, e, r),
                    scalar1=row_scale[g][:, k : k + 1],
                    scalar2=None,
                    op0=ALU.mult,
                )

        def transpose_rows(g, j):
            e, h = divmod(j, 2)
            e_words = e_norm[g][:].bitcast(F32)
            et_ps[g, j] = psum.tile([P, 2, 2 * P], F32, name="et_ps", tag="bank")
            for rr in range(2):
                for u in range(2):
                    nc.tensor.transpose(
                        out=et_ps[g, j][:, u, rr * P : (rr + 1) * P],
                        in_=e_words[:, e, 2 * h + rr, u * P : (u + 1) * P],
                        identity=ident_f32[:],
                    )

        def regroup_edges(g, j):
            e, h = divmod(j, 2)
            if j == 0:
                e_grouped[g] = pipe2.tile([P, KINDS, N * PACK], BF16, name="e_grouped", align_bytes=64)
            e_grouped_words = e_grouped[g][:].bitcast(F32)
            copy_out = nc.vector.tensor_copy if g < FILL_GRAPHS else nc.scalar.copy
            copy_out(
                out=e_grouped_words[:, e, h * 4 * P : (h + 1) * 4 * P].rearrange(
                    "p (n u) -> p n u", u=2
                ),
                in_=et_ps[g, j][:].rearrange("p u n -> p n u"),
            )

        def quantise_edges(g, e):
            if e == 0:
                e_codes[g] = pipe2.tile([P, KINDS, N], U32, name="e_codes", align_bytes=64)
                e_scales[g] = pipe2.tile([P, KINDS, N], U8, name="e_scales", align_bytes=64)
            nc.vector.quantize_mx(
                out=e_codes[g][:, e, :].bitcast(FP8X4),
                scales=e_scales[g][:, e, :],
                in_=e_grouped[g][:, e, :],
            )

        def x_matmul(g, nb):
            xt_ps[g, nb] = psum.tile([P, PACK, P], F32, name="xt_ps", tag="bank")
            for e in range(KINDS):
                for dh in range(2):
                    nc.tensor.matmul_mx(
                        out=xt_ps[g, nb][:, 2 * e + dh, :],
                        lhsT=p_codes[g][:, dh * P : (dh + 1) * P].bitcast(FP8X4),
                        lhsT_scale=p_scales[g][:, dh * P : (dh + 1) * P],
                        rhs=e_codes[g][:, e, nb * P : (nb + 1) * P].bitcast(FP8X4),
                        rhs_scale=e_scales[g][:, e, nb * P : (nb + 1) * P],
                        start=True,
                        stop=True,
                    )

        def regroup_x(g, nb):
            if nb == 0:
                x_grouped[g] = pipe2.tile([P, N, PACK], BF16, name="x_grouped", align_bytes=64)
            on_scalar = nb != 2 or g >= B - DRAIN_GRAPHS
            copy_out = nc.scalar.copy if on_scalar else nc.vector.tensor_copy
            copy_out(
                out=x_grouped[g][:, nb * P : (nb + 1) * P, :],
                in_=xt_ps[g, nb][:].rearrange("p t n -> p n t"),
            )

        def quantise_x(g):
            nc.vector.quantize_mx(
                out=x_codes[:, g, :].bitcast(FP8X4),
                scales=x_scales[:, g, :],
                in_=x_grouped[g][:].rearrange("p n t -> p (n t)"),
            )

        def z_first(g, ob):
            z_ps[g, ob] = z_matmul(g, ob)

        def z_statistics(g, ob):
            nc.vector.bn_stats(out=stats[:, ob, g, :], in_=z_ps[g, ob][:])

        bn_scale, bn_shift, bn_parts = {}, {}, {}

        def start_batch_norm(obs):
            count = len(obs)
            mean_var = const.tile([P, count, 2], F32, name="mean_var_%d" % count)
            for i, ob in enumerate(obs):
                nc.vector.bn_aggr(
                    out=mean_var[:, i, :], in_=stats[:, ob, :, :].rearrange("p g s -> p (g s)")
                )
            std = const.tile([P, count], F32, name="std_%d" % count)
            nc.scalar.activation(
                out=std[:], in_=mean_var[:, :, 1], func=ACT.Sqrt, bias=EPS_BN, scale=1.0
            )
            gain_mean = const.tile([P, count], F32, name="gain_mean_%d" % count)
            nc.vector.tensor_mul(
                out=gain_mean[:], in0=gb_cols[:, obs[0] : obs[0] + count], in1=mean_var[:, :, 0]
            )
            bn_parts[count] = (std, gain_mean)

        def finish_batch_norm(obs):
            count = len(obs)
            std, gain_mean = bn_parts[count]
            inv_std = const.tile([P, count], F32, name="inv_std_%d" % count)
            nc.vector.reciprocal(out=inv_std[:], in_=std[:])
            mean_scaled = const.tile([P, count], F32, name="mean_scaled_%d" % count)
            nc.vector.tensor_mul(out=mean_scaled[:], in0=gain_mean[:], in1=inv_std[:])
            scale = const.tile([P, count], F32, name="bn_scale_%d" % count)
            nc.vector.tensor_mul(
                out=scale[:], in0=gb_cols[:, obs[0] : obs[0] + count], in1=inv_std[:]
            )
            shift = const.tile([P, count], F32, name="bn_shift_%d" % count)
            first_b = QUARTERS + obs[0]
            nc.vector.tensor_sub(
                out=shift[:], in0=gb_cols[:, first_b : first_b + count], in1=mean_scaled[:]
            )
            for i, ob in enumerate(obs):
                bn_scale[ob] = scale[:, i : i + 1]
                bn_shift[ob] = shift[:, i : i + 1]

        def due(step, first_step):
            g, q = divmod(step - first_step, QUARTERS)
            return (g, q) if 0 <= g < B else (None, q)

        for step in range(EDGE_LOAD_AT, LAST_STEP + 1):
            g, q = due(step, ROW_SCALE_AT)
            if g is not None and q == 0:
                clamp_row_sums(g)
            g, q = due(step, P_QUANT_AT)
            if g is not None and q % 2 == 0:
                quantise_nodes(g, q // 2)
            g, q = due(step, P_REGROUP_AT)
            if g is not None and q % 2 == 0:
                regroup_nodes(g, q // 2)
            g, q = due(step, Z_STATS_AT)
            if g is not None:
                z_statistics(g, q)
            if g == B - 1:
                if q == 0:
                    start_batch_norm(HEAD_BLOCKS)
                elif q == 1:
                    finish_batch_norm(HEAD_BLOCKS)
                elif q == QUARTERS - 1:
                    start_batch_norm(OTHER_BLOCKS)
                    finish_batch_norm(OTHER_BLOCKS)
            g, q = due(step, ABS_AT)
            if g is not None:
                sum_rows_on_vector(g, q)
            g, q = due(step, Z_MATMUL_AT)
            if g is not None:
                z_first(g, q)
            g, q = due(step, X_QUANT_AT)
            if g is not None and q == 0:
                quantise_x(g)
            g, q = due(step, X_REGROUP_AT)
            if g is not None:
                regroup_x(g, q)
            g, q = due(step, X_MATMUL_AT)
            if g is not None:
                x_matmul(g, q)
            g, q = due(step, E_QUANT_AT)
            if g is not None and q % 2 == 0:
                quantise_edges(g, q // 2)
            g, q = due(step, E_REGROUP_AT)
            if g is not None:
                regroup_edges(g, q)
            g, q = due(step, TRANSPOSE_AT)
            if g is not None:
                transpose_rows(g, q)
            g, q = due(step, NORM_AT)
            if g is not None:
                normalise_rows(g, q)
            g, q = due(step, ABS_AT)
            if g is not None:
                sum_rows_on_scalar(g, q)
            if step == WEIGHTS_STEP:
                prepare_weights()
            g, q = due(step, MASK_AT)
            if g == 0:
                mask_diagonals(g, slice(q, q + 1))
            elif g is not None and q == 0:
                mask_diagonals(g, slice(0, QUARTERS))
            g, q = due(step, ROW_SCALE_AT)
            if g is not None and q == 0:
                invert_row_sums(g)
            g, q = due(step, EDGE_LOAD_AT)
            if g is not None and q == 0:
                load_edges(g)
            g, q = due(step, NODE_LOAD_AT)
            if g is not None and q == 0:
                load_nodes(g)
                if g == 0:
                    load_weights()

        ys = {}

        def second_pass(g, blocks, parts=1):
            if g not in ys:
                ys[g] = pipe6.tile([P, QUARTERS, N], F32, name="y")
            y = ys[g]
            z_banks = [z_matmul(g, ob) for ob in blocks]
            run = slice(blocks[0], blocks[-1] + 1)
            for i in range(parts):
                cols = slice(i * (N // parts), (i + 1) * (N // parts))
                for z_again, ob in zip(z_banks, blocks):
                    nc.scalar.activation(
                        out=y[:, ob, cols],
                        in_=z_again[:, cols],
                        func=ACT.Identity,
                        scale=bn_scale[ob],
                        bias=bn_shift[ob],
                    )
                nc.vector.scalar_tensor_tensor(
                    out=y[:, run, cols],
                    in0=y[:, run, cols],
                    scalar=NEG_SLOPE,
                    in1=y[:, run, cols],
                    op0=ALU.mult,
                    op1=ALU.max,
                )
                nc.sync.dma_start(
                    out=out[g].rearrange("(p ob) n -> p ob n", p=P)[:, run, cols],
                    in_=y[:, run, cols],
                )

        for g in range(HEAD_GRAPHS):
            second_pass(g, HEAD_BLOCKS)
        for g in range(HEAD_GRAPHS):
            second_pass(g, [1])
            second_pass(g, [2, 3])
        for g in range(HEAD_GRAPHS, B - 1):
            second_pass(g, [0, 1])
            second_pass(g, [2, 3])
        for ob in range(QUARTERS - 1):
            second_pass(B - 1, [ob])
        second_pass(B - 1, [QUARTERS - 1], parts=2)
